import numpy as np
import ml_dtypes


def mxq(x, axis, fmt="e4m3"):
    dtype, down = {"e4m3": (ml_dtypes.float8_e4m3fn, 7), "e5m2": (ml_dtypes.float8_e5m2, 14)}[fmt]
    v = np.moveaxis(np.asarray(x, np.float32).astype(ml_dtypes.bfloat16).astype(np.float64), axis, -1)
    blocks = v.reshape(v.shape[:-1] + (-1, 32))
    amax = np.abs(blocks).max(-1, keepdims=True)
    byte = np.maximum(np.where(amax > 0, np.frexp(amax)[1] - 1 + 127, 0) - down, 1)
    scale = np.exp2(byte - 127.0)
    codes = (blocks / scale).astype(np.float32).astype(dtype).astype(np.float64)
    return np.moveaxis((codes * scale).reshape(v.shape), -1, axis)


WIDE = False


def mx_kscale(k):
    if not WIDE:
        return np.ones(k)
    levels = np.array([10, -10, 5, -5, 0])
    a = np.random.permutation(np.resize(levels, k // 512 * 4)).reshape(k // 512, 4)
    idx = np.arange(k)
    return np.exp2(a[idx // 512, idx % 128 // 32])


BF16 = ml_dtypes.bfloat16


def bf(x):
    return np.asarray(x, np.float32).astype(BF16)


def f64(x):
    return np.asarray(x).astype(np.float64)


B, S, H, NH, QB = 1, 1024, 1024, 8, 512
D = H // NH
MASKED = -10000.0


def alibi_slopes():
    base = 2.0 ** (-(2.0 ** -(np.log2(NH) - 3.0)))
    return base ** np.arange(1, 1 + NH)


def setup_inputs():
    s = mx_kscale(H)
    return {"q": bf(np.random.standard_normal((B, S, NH, D))),
            "k": bf(np.random.standard_normal((B, S, NH, D))),
            "hidden_states": bf(np.random.standard_normal((B, S, H)) * s),
            "w_v": bf(np.random.standard_normal((H, H)) / np.sqrt(H) / s[None, :]),
            "b_v": bf(np.random.standard_normal(H) * 0.2)}


def reference(q, k, hidden_states, w_v, b_v):
    qt = f64(q).transpose(0, 2, 1, 3)
    kt = f64(k).transpose(0, 2, 3, 1)
    v = (mxq(f64(hidden_states), 2, "e4m3") @ mxq(f64(w_v), 1, "e4m3").T) + f64(b_v)
    vq = mxq(v.reshape(B, S, NH, D).transpose(0, 2, 1, 3), 2, "e4m3")
    slopes = alibi_slopes()
    pos = np.arange(S)
    blocks = []
    for q0 in range(0, S, QB):
        n = q0 + QB
        s = qt[:, :, q0:n] @ kt[:, :, :, :n] / np.sqrt(D) + slopes[None, :, None, None] * pos[None, None, None, :n]
        causal = pos[None, :n] <= pos[q0:n, None]
        s = np.where(causal, s, MASKED)
        e = np.exp(s - s.max(-1, keepdims=True)) * causal
        blocks.append((mxq(e, 3, "e4m3") @ vq[:, :, :n]) / e.sum(-1, keepdims=True))
    return np.concatenate(blocks, axis=2).transpose(0, 2, 1, 3).reshape(B, S, H)

@@ -1,0 +1,293 @@
+import math
+from contextlib import ExitStack
+
+import concourse.mybir as mybir
+from concourse.masks import make_identity
+
+F32 = mybir.dt.float32
+BF16 = mybir.dt.bfloat16
+I32 = mybir.dt.int32
+U32 = mybir.dt.uint32
+U8 = mybir.dt.uint8
+FP8X4 = mybir.dt.float8_e4m3fn_x4
+ALU = mybir.AluOpType
+ACT = mybir.ActivationFunctionType
+AXIS = mybir.AxisListType
+
+P = 128
+PACK = 4
+SPAN = P * PACK
+SEQ = 1024
+HIDDEN = 1024
+HEADS = 8
+D = HIDDEN // HEADS
+Q_TILES = SEQ // P
+SPANS = SEQ // SPAN
+BLOCKS = SPAN // P
+HALF = P // 2
+
+SCALE = 1.0 / math.sqrt(D)
+MASKED = -10000.0
+
+FLOPS = 2 * SEQ * HIDDEN * HIDDEN + 2 * (2 * HEADS * D * (SPAN * SPAN + SPAN * SEQ))
+
+
+def place_of(a, g):
+    if a < BLOCKS:
+        return a // 2, a % 2
+    return a - 2, g
+
+
+def blocks_seen(a, g):
+    return min(a + 1 - BLOCKS * g, BLOCKS)
+
+
+def tile_bloomattention_pa_kernel(tc, q, k, hidden_states, w_v, b_v, out):
+    nc = tc.nc
+    with ExitStack() as ctx:
+        inputs = ctx.enter_context(tc.tile_pool(name="inputs", bufs=1))
+        consts = ctx.enter_context(tc.tile_pool(name="consts", bufs=1))
+        operands = ctx.enter_context(tc.tile_pool(name="operands", bufs=1))
+        e_pool = ctx.enter_context(tc.tile_pool(name="e_pool", bufs=1))
+        turned_heads = ctx.enter_context(tc.tile_pool(name="turned_heads", bufs=2))
+        stage = ctx.enter_context(tc.tile_pool(name="stage", bufs=4))
+        e_operands = ctx.enter_context(tc.tile_pool(name="e_operands", bufs=8))
+        small = ctx.enter_context(tc.tile_pool(name="small", bufs=6))
+        results = ctx.enter_context(tc.tile_pool(name="results", bufs=4))
+        psum_scores = ctx.enter_context(tc.psum_pool(name="psum_scores", bufs=4))
+        psum_turned = ctx.enter_context(tc.psum_pool(name="psum_turned", bufs=2))
+        psum_products = ctx.enter_context(tc.psum_pool(name="psum_products", bufs=2))
+
+        k_sb = inputs.tile([P, 2 * SPANS, 2, HIDDEN], BF16)
+        k_rows = k.rearrange("b (c y u) h d -> y (b c) u (h d)", y=P, u=2)
+        q_sb = inputs.tile([P, Q_TILES, HIDDEN], BF16)
+        q_rows = q.rearrange("b (a p) h d -> p (b a) (h d)", p=P)
+        hs_sb = inputs.tile([P, SPANS, PACK, HIDDEN], BF16)
+        hs_rows = hidden_states.rearrange("b (g p s) f -> p (b g) s f", p=P, s=PACK)
+        w_sb = inputs.tile([P, HEADS, HIDDEN], BF16)
+        w_rows = w_v.rearrange("(o p) f -> p o f", p=P)
+        nc.sync.dma_start(out=k_sb[:, 0:2], in_=k_rows[:, 0:2])
+        nc.sync.dma_start(out=q_sb[:, 0:4], in_=q_rows[:, 0:4])
+        nc.sync.dma_start(out=k_sb[:, 2:4], in_=k_rows[:, 2:4])
+        nc.sync.dma_start(out=q_sb[:, 4:8], in_=q_rows[:, 4:8])
+        nc.sync.dma_start(out=hs_sb[:, 0:1], in_=hs_rows[:, 0:1])
+        nc.sync.dma_start(out=hs_sb[:, 1:2], in_=hs_rows[:, 1:2])
+        nc.sync.dma_start(out=w_sb[:, 0:4], in_=w_rows[:, 0:4])
+        nc.sync.dma_start(out=w_sb[:, 4:8], in_=w_rows[:, 4:8])
+        bias_sb = inputs.tile([P, HIDDEN], BF16)
+        nc.scalar.dma_start(out=bias_sb[:], in_=b_v.partition_broadcast(P))
+
+        ident_bf = consts.tile([P, P], BF16)
+        make_identity(nc, ident_bf[:])
+        ident_f32 = consts.tile([P, P], F32)
+        make_identity(nc, ident_f32[:])
+
+        position_i32 = consts.tile([P, Q_TILES], I32)
+        ahead_i32 = consts.tile([P, P], I32)
+        for u in range(2):
+            plane = slice(HALF * u, HALF * (u + 1))
+            nc.gpsimd.iota(
+                position_i32[plane, :], pattern=[[-P, Q_TILES]], base=u - (P - 1), channel_multiplier=2
+            )
+            nc.gpsimd.iota(ahead_i32[plane, :], pattern=[[1, P]], base=-u, channel_multiplier=-2)
+        position = consts.tile([P, Q_TILES], F32)
+        nc.vector.tensor_copy(out=position[:], in_=position_i32[:])
+        mask = consts.tile([P, P], F32)
+        nc.vector.tensor_scalar(
+            out=mask[:], in0=ahead_i32[:], scalar1=0.0, scalar2=MASKED / SCALE, op0=ALU.is_lt, op1=ALU.mult
+        )
+        slope_term = consts.tile([P, HEADS, Q_TILES], F32)
+        diagonal_term = consts.tile([P, HEADS, P], F32)
+        for h in range(HEADS):
+            slope = 0.5 ** (h + 1)
+            nc.vector.tensor_scalar_mul(out=slope_term[:, h, :], in0=position[:], scalar1=slope / SCALE)
+            nc.vector.tensor_scalar(
+                out=diagonal_term[:, h, :], in0=mask[:], scalar1=slope_term[:, h, 0:1], scalar2=None, op0=ALU.add
+            )
+
+        e_tiles = []
+        for parity in range(2):
+            e_tiles.append([])
+            for t in range(6):
+                e_tiles[parity].append(e_pool.tile([P, 2, 2, 2 * P], BF16, name="e_%d_%d" % (parity, t)))
+            for a in range(Q_TILES):
+                g = a // BLOCKS
+                t, half = place_of(a, g)
+                unseen = HALF * blocks_seen(a, g)
+                if unseen < 2 * P:
+                    nc.vector.memset(e_tiles[parity][t][:, half, :, unseen:], 0.0)
+
+        hs_words = operands.tile([P, SPANS, PACK, SPANS, P], U32, align_bytes=64)
+        hs_scales = operands.tile([P, SPANS, PACK, SPANS, P], U8, align_bytes=64)
+        w_words = operands.tile([P, HEADS, SPANS, P], U32, align_bytes=64)
+        w_scales = operands.tile([P, HEADS, SPANS, P], U8, align_bytes=64)
+        v_words = operands.tile([P, HEADS, SPANS, D], U32, align_bytes=64)
+        v_scales = operands.tile([P, HEADS, SPANS, D], U8, align_bytes=64)
+
+        def quantise_rows(rows, words, scales):
+            pairs = rows.bitcast(F32)
+            turned = psum_turned.tile([P, 2, 2, P], F32, tag="turned")
+            for c in range(2):
+                for u in range(2):
+                    first = (2 * c + u) * P
+                    nc.tensor.transpose(turned[:, c, u, :], pairs[:, first : first + P], ident_f32[:])
+            grouped = stage.tile([P, 2, P, PACK], BF16, tag="grouped", align_bytes=64)
+            nc.scalar.copy(out=grouped[:].bitcast(F32), in_=turned[:].rearrange("p c u r -> p c r u"))
+            nc.vector.quantize_mx(
+                out=words.rearrange("p c r -> p (c r)").bitcast(FP8X4),
+                scales=scales.rearrange("p c r -> p (c r)"),
+                in_=grouped[:].rearrange("p c r s -> p (c r s)"),
+            )
+
+        def turn_q_and_k(h):
+            head = slice(h * D, (h + 1) * D)
+            q_turned = psum_turned.tile([P, Q_TILES, P], BF16, tag="turned")
+            for a in range(Q_TILES):
+                nc.tensor.transpose(q_turned[:, a, :], q_sb[:, a, head], ident_bf[:])
+            qT = turned_heads.tile([P, Q_TILES, P], BF16, tag="qT")
+            nc.scalar.copy(out=qT[:], in_=q_turned[:])
+            k_turned = psum_turned.tile([P, SPANS, 2, 2, P], BF16, tag="turned")
+            for c in range(2 * SPANS):
+                for u in range(2):
+                    nc.tensor.transpose(k_turned[:, c // 2, u, c % 2, :], k_sb[:, c, u, head], ident_bf[:])
+            kT = turned_heads.tile([P, SPANS, 2, 2 * P], BF16, tag="kT")
+            nc.scalar.copy(out=kT[:], in_=k_turned[:].rearrange("p g u f y -> p g u (f y)"))
+            return qT, kT
+
+        def project_v(h):
+            head = slice(h * D, (h + 1) * D)
+            grouped = stage.tile([P, SPANS, D, PACK], BF16, tag="grouped", align_bytes=64)
+            for g in range(SPANS):
+                product = psum_products.tile([P, PACK, D], F32, tag="product")
+                for slot in range(PACK):
+                    s = 2 * (slot % 2) + slot // 2
+                    for c in range(SPANS):
+                        nc.tensor.matmul_mx(
+                            out=product[:, slot, :],
+                            lhsT=hs_words[:, g, s, c, :].bitcast(FP8X4),
+                            lhsT_scale=hs_scales[:, g, s, c, :],
+                            rhs=w_words[:, h, c, :].bitcast(FP8X4),
+                            rhs_scale=w_scales[:, h, c, :],
+                            start=(c == 0),
+                            stop=(c == SPANS - 1),
+                        )
+                nc.vector.tensor_tensor(
+                    out=grouped[:, g, :, :],
+                    in0=product[:].rearrange("p s d -> p d s"),
+                    in1=bias_sb[:, head].unsqueeze(2).to_broadcast([P, D, PACK]),
+                    op=ALU.add,
+                )
+            nc.vector.quantize_mx(
+                out=v_words[:, h].rearrange("p g d -> p (g d)").bitcast(FP8X4),
+                scales=v_scales[:, h].rearrange("p g d -> p (g d)"),
+                in_=grouped[:].rearrange("p g d s -> p (g d s)"),
+            )
+
+        def softmax_rows(h, a, qT, kT, sums):
+            spans = a // BLOCKS + 1
+            tops = small.tile([P, SPANS], F32, tag="tops")
+            banks = []
+            for g in range(spans):
+                blocks = blocks_seen(a, g)
+                width = HALF * blocks
+                bank = psum_scores.tile([P, 2, 2 * P], F32, tag="scores")
+                for block in range(blocks):
+                    behind = a - (BLOCKS * g + block)
+                    if behind == 0:
+                        term = diagonal_term[:, h, :]
+                    else:
+                        term = slope_term[:, h, behind : behind + 1].to_broadcast([P, P])
+                    nc.tensor.matmul(
+                        out=bank[:, :, HALF * block : HALF * (block + 1)],
+                        lhsT=term,
+                        rhs=ident_f32[:].rearrange("p (u z) -> p u z", u=2),
+                        is_transpose=True,
+                        start=(block == 0),
+                        stop=False,
+                    )
+                nc.tensor.matmul(
+                    out=bank[:, :, 0:width], lhsT=qT[:, a, :], rhs=kT[:, g, :, 0:width], start=False, stop=True
+                )
+                nc.vector.tensor_reduce(out=tops[:, g : g + 1], in_=bank[:, :, 0:width], axis=AXIS.XY, op=ALU.max)
+                banks.append(bank)
+            shift = small.tile([P, 1], F32, tag="shift")
+            if spans == 1:
+                nc.vector.tensor_scalar_mul(out=shift[:], in0=tops[:, 0:1], scalar1=-SCALE)
+            else:
+                nc.vector.tensor_scalar(
+                    out=shift[:], in0=tops[:, 0:1], scalar1=tops[:, 1:2], scalar2=-SCALE, op0=ALU.max, op1=ALU.mult
+                )
+            for g in range(spans):
+                width = HALF * blocks_seen(a, g)
+                t, half = place_of(a, g)
+                nc.scalar.activation(
+                    out=e_tiles[h % 2][t][:, half, :, 0:width],
+                    in_=banks[g][:, :, 0:width],
+                    func=ACT.Exp,
+                    bias=shift[:, 0:1],
+                    scale=SCALE,
+                    accum_out=sums[:, g, a : a + 1],
+                )
+
+        def quantise_e(h, t):
+            words = e_operands.tile([P, 2, P], U32, tag="e_words", align_bytes=64)
+            scales = e_operands.tile([P, 2, P], U8, tag="e_scales", align_bytes=64)
+            quantise_rows(e_tiles[h % 2][t][:].rearrange("p n u z -> p (n u z)"), words[:], scales[:])
+            return words, scales
+
+        def attend(h, upper, e_mx, sums):
+            first = BLOCKS * upper
+            product = psum_products.tile([P, BLOCKS, D], F32, tag="product")
+            for j in range(BLOCKS):
+                for g in range(upper + 1):
+                    t, half = place_of(first + j, g)
+                    words, scales = e_mx[t]
+                    nc.tensor.matmul_mx(
+                        out=product[:, j, :],
+                        lhsT=words[:, half, :].bitcast(FP8X4),
+                        lhsT_scale=scales[:, half, :],
+                        rhs=v_words[:, h, g, :].bitcast(FP8X4),
+                        rhs_scale=v_scales[:, h, g, :],
+                        start=(g == 0),
+                        stop=(g == upper),
+                    )
+            inverse = small.tile([P, BLOCKS], F32, tag="inverse")
+            if upper == 0:
+                nc.vector.reciprocal(out=inverse[:], in_=sums[:, 0, 0:BLOCKS])
+            else:
+                total = small.tile([P, BLOCKS], F32, tag="total")
+                nc.vector.tensor_tensor(out=total[:], in0=sums[:, 0, first:], in1=sums[:, 1, first:], op=ALU.add)
+                nc.vector.reciprocal(out=inverse[:], in_=total[:])
+            result = results.tile([P, BLOCKS, D], F32, tag="result")
+            nc.vector.tensor_tensor(
+                out=result[:],
+                in0=product[:],
+                in1=inverse[:].unsqueeze(2).to_broadcast([P, BLOCKS, D]),
+                op=ALU.mult,
+            )
+            nc.sync.dma_start(out=out_rows[:, first : first + BLOCKS, h, :], in_=result[:])
+
+        out_rows = out.rearrange("b (a p) (h d) -> p (b a) h d", p=P, d=D)
+
+        qT, kT = turn_q_and_k(0)
+        for h in range(HEADS):
+            sums = small.tile([P, SPANS, Q_TILES], F32, tag="sums")
+            e_mx = {}
+            for a in range(BLOCKS):
+                softmax_rows(h, a, qT, kT, sums)
+                if a % 2 == 1:
+                    e_mx[a // 2] = quantise_e(h, a // 2)
+            if h == 0:
+                for g in range(SPANS):
+                    for s in range(PACK):
+                        quantise_rows(hs_sb[:, g, s, :], hs_words[:, g, s], hs_scales[:, g, s])
+            quantise_rows(w_sb[:, h, :], w_words[:, h], w_scales[:, h])
+            project_v(h)
+            attend(h, 0, e_mx, sums)
+            following = turn_q_and_k(h + 1) if h + 1 < HEADS else None
+            for a in range(BLOCKS, Q_TILES):
+                softmax_rows(h, a, qT, kT, sums)
+                e_mx[a - 2] = quantise_e(h, a - 2)
+            attend(h, 1, e_mx, sums)
+            if following is not None:
+                qT, kT = following

@@ -32,10 +32,12 @@ MASKED = -10000.0
 FLOPS = 2 * SEQ * HIDDEN * HIDDEN + 2 * (2 * HEADS * D * (SPAN * SPAN + SPAN * SEQ))
 
 
-def place_of(a, g):
-    if a < BLOCKS:
-        return a // 2, a % 2
-    return a - 2, g
+LAG_TURN = 2
+LAG_QUANTISE = 3
+
+
+def spans_seen(a):
+    return a // BLOCKS + 1
 
 
 def blocks_seen(a, g):
@@ -45,13 +47,14 @@ def blocks_seen(a, g):
 def tile_bloomattention_pa_kernel(tc, q, k, hidden_states, w_v, b_v, out):
     nc = tc.nc
     with ExitStack() as ctx:
+        ctx.enter_context(tc.manual_schedule())
         inputs = ctx.enter_context(tc.tile_pool(name="inputs", bufs=1))
         consts = ctx.enter_context(tc.tile_pool(name="consts", bufs=1))
         operands = ctx.enter_context(tc.tile_pool(name="operands", bufs=1))
         e_pool = ctx.enter_context(tc.tile_pool(name="e_pool", bufs=1))
-        turned_heads = ctx.enter_context(tc.tile_pool(name="turned_heads", bufs=2))
+        turned_heads = ctx.enter_context(tc.tile_pool(name="turned_heads", bufs=4))
         stage = ctx.enter_context(tc.tile_pool(name="stage", bufs=4))
-        e_operands = ctx.enter_context(tc.tile_pool(name="e_operands", bufs=8))
+        e_operands = ctx.enter_context(tc.tile_pool(name="e_operands", bufs=12))
         small = ctx.enter_context(tc.tile_pool(name="small", bufs=6))
         results = ctx.enter_context(tc.tile_pool(name="results", bufs=4))
         psum_scores = ctx.enter_context(tc.psum_pool(name="psum_scores", bufs=4))
@@ -76,6 +79,7 @@ def tile_bloomattention_pa_kernel(tc, q, k, hidden_states, w_v, b_v, out):
         nc.sync.dma_start(out=w_sb[:, 4:8], in_=w_rows[:, 4:8])
         bias_sb = inputs.tile([P, HIDDEN], BF16)
         nc.scalar.dma_start(out=bias_sb[:], in_=b_v.partition_broadcast(P))
+        out_rows = out.rearrange("b (a p) (h d) -> p (b a) h d", p=P, d=D)
 
         ident_bf = consts.tile([P, P], BF16)
         make_identity(nc, ident_bf[:])
@@ -90,6 +94,18 @@ def tile_bloomattention_pa_kernel(tc, q, k, hidden_states, w_v, b_v, out):
                 position_i32[plane, :], pattern=[[-P, Q_TILES]], base=u - (P - 1), channel_multiplier=2
             )
             nc.gpsimd.iota(ahead_i32[plane, :], pattern=[[1, P]], base=-u, channel_multiplier=-2)
+
+        e_tiles = []
+        for parity in range(2):
+            e_tiles.append([])
+            for a in range(Q_TILES):
+                e_tile = e_pool.tile([P, spans_seen(a), 2, 2 * P], BF16, name="e_%d_%d" % (parity, a))
+                e_tiles[parity].append(e_tile)
+                last = spans_seen(a) - 1
+                unseen = HALF * blocks_seen(a, last)
+                if unseen < 2 * P:
+                    nc.vector.memset(e_tile[:, last, :, unseen:], 0.0)
+
         position = consts.tile([P, Q_TILES], F32)
         nc.vector.tensor_copy(out=position[:], in_=position_i32[:])
         mask = consts.tile([P, P], F32)
@@ -105,18 +121,6 @@ def tile_bloomattention_pa_kernel(tc, q, k, hidden_states, w_v, b_v, out):
                 out=diagonal_term[:, h, :], in0=mask[:], scalar1=slope_term[:, h, 0:1], scalar2=None, op0=ALU.add
             )
 
-        e_tiles = []
-        for parity in range(2):
-            e_tiles.append([])
-            for t in range(6):
-                e_tiles[parity].append(e_pool.tile([P, 2, 2, 2 * P], BF16, name="e_%d_%d" % (parity, t)))
-            for a in range(Q_TILES):
-                g = a // BLOCKS
-                t, half = place_of(a, g)
-                unseen = HALF * blocks_seen(a, g)
-                if unseen < 2 * P:
-                    nc.vector.memset(e_tiles[parity][t][:, half, :, unseen:], 0.0)
-
         hs_words = operands.tile([P, SPANS, PACK, SPANS, P], U32, align_bytes=64)
         hs_scales = operands.tile([P, SPANS, PACK, SPANS, P], U8, align_bytes=64)
         w_words = operands.tile([P, HEADS, SPANS, P], U32, align_bytes=64)
@@ -124,35 +128,55 @@ def tile_bloomattention_pa_kernel(tc, q, k, hidden_states, w_v, b_v, out):
         v_words = operands.tile([P, HEADS, SPANS, D], U32, align_bytes=64)
         v_scales = operands.tile([P, HEADS, SPANS, D], U8, align_bytes=64)
 
-        def quantise_rows(rows, words, scales):
+        def turn_rows(rows, count, copy_out):
             pairs = rows.bitcast(F32)
-            turned = psum_turned.tile([P, 2, 2, P], F32, tag="turned")
-            for c in range(2):
+            turned = psum_turned.tile([P, count, 2, P], F32, tag="turned")
+            for c in range(count):
                 for u in range(2):
                     first = (2 * c + u) * P
                     nc.tensor.transpose(turned[:, c, u, :], pairs[:, first : first + P], ident_f32[:])
-            grouped = stage.tile([P, 2, P, PACK], BF16, tag="grouped", align_bytes=64)
-            nc.scalar.copy(out=grouped[:].bitcast(F32), in_=turned[:].rearrange("p c u r -> p c r u"))
+            grouped = stage.tile([P, count, P, PACK], BF16, tag="grouped", align_bytes=64)
+            copy_out(out=grouped[:].bitcast(F32), in_=turned[:].rearrange("p c u r -> p c r u"))
+            return grouped
+
+        def quantise(grouped, words, scales):
             nc.vector.quantize_mx(
                 out=words.rearrange("p c r -> p (c r)").bitcast(FP8X4),
                 scales=scales.rearrange("p c r -> p (c r)"),
                 in_=grouped[:].rearrange("p c r s -> p (c r s)"),
             )
 
-        def turn_q_and_k(h):
+        def quantise_w(h):
+            quantise(turn_rows(w_sb[:, h, :], SPANS, nc.scalar.copy), w_words[:, h], w_scales[:, h])
+
+        def quantise_hidden_states():
+            for g in range(SPANS):
+                for s in range(PACK):
+                    copy_out = nc.scalar.copy if s % 2 == 0 else nc.vector.tensor_copy
+                    grouped = turn_rows(hs_sb[:, g, s, :], SPANS, copy_out)
+                    quantise(grouped, hs_words[:, g, s], hs_scales[:, g, s])
+
+        qk_turned = {}
+
+        def turn_q_and_k(h, half):
             head = slice(h * D, (h + 1) * D)
-            q_turned = psum_turned.tile([P, Q_TILES, P], BF16, tag="turned")
-            for a in range(Q_TILES):
-                nc.tensor.transpose(q_turned[:, a, :], q_sb[:, a, head], ident_bf[:])
-            qT = turned_heads.tile([P, Q_TILES, P], BF16, tag="qT")
-            nc.scalar.copy(out=qT[:], in_=q_turned[:])
-            k_turned = psum_turned.tile([P, SPANS, 2, 2, P], BF16, tag="turned")
-            for c in range(2 * SPANS):
-                for u in range(2):
-                    nc.tensor.transpose(k_turned[:, c // 2, u, c % 2, :], k_sb[:, c, u, head], ident_bf[:])
-            kT = turned_heads.tile([P, SPANS, 2, 2 * P], BF16, tag="kT")
-            nc.scalar.copy(out=kT[:], in_=k_turned[:].rearrange("p g u f y -> p g u (f y)"))
-            return qT, kT
+            turned = psum_turned.tile([P, 2, BLOCKS, P], BF16, tag="turned")
+            for j in range(BLOCKS):
+                nc.tensor.matmul(
+                    out=turned[:, 0, j, :], lhsT=q_sb[:, BLOCKS * half + j, head], rhs=ident_bf[:], start=True, stop=True
+                )
+            for u in range(2):
+                for f in range(2):
+                    nc.tensor.matmul(
+                        out=turned[:, 1, 2 * u + f, :],
+                        lhsT=k_sb[:, 2 * half + f, u, head],
+                        rhs=ident_bf[:],
+                        start=True,
+                        stop=True,
+                    )
+            qk = turned_heads.tile([P, 2, BLOCKS, P], BF16, tag="qk")
+            nc.scalar.copy(out=qk[:], in_=turned[:])
+            qk_turned[(h, half)] = qk
 
         def project_v(h):
             head = slice(h * D, (h + 1) * D)
@@ -177,17 +201,17 @@ def tile_bloomattention_pa_kernel(tc, q, k, hidden_states, w_v, b_v, out):
                     in1=bias_sb[:, head].unsqueeze(2).to_broadcast([P, D, PACK]),
                     op=ALU.add,
                 )
-            nc.vector.quantize_mx(
-                out=v_words[:, h].rearrange("p g d -> p (g d)").bitcast(FP8X4),
-                scales=v_scales[:, h].rearrange("p g d -> p (g d)"),
-                in_=grouped[:].rearrange("p g d s -> p (g d s)"),
-            )
+            quantise(grouped, v_words[:, h], v_scales[:, h])
 
-        def softmax_rows(h, a, qT, kT, sums):
-            spans = a // BLOCKS + 1
+        row_sums = {}
+        scored = {}
+        e_grouped = {}
+        e_mx = {}
+
+        def scores(h, a):
             tops = small.tile([P, SPANS], F32, tag="tops")
             banks = []
-            for g in range(spans):
+            for g in range(spans_seen(a)):
                 blocks = blocks_seen(a, g)
                 width = HALF * blocks
                 bank = psum_scores.tile([P, 2, 2 * P], F32, tag="scores")
@@ -206,51 +230,62 @@ def tile_bloomattention_pa_kernel(tc, q, k, hidden_states, w_v, b_v, out):
                         stop=False,
                     )
                 nc.tensor.matmul(
-                    out=bank[:, :, 0:width], lhsT=qT[:, a, :], rhs=kT[:, g, :, 0:width], start=False, stop=True
+                    out=bank[:, :, 0:width],
+                    lhsT=qk_turned[(h, a // BLOCKS)][:, 0, a % BLOCKS, :],
+                    rhs=qk_turned[(h, g)][:, 1].rearrange("p (u f) y -> p u (f y)", u=2)[:, :, 0:width],
+                    start=False,
+                    stop=True,
                 )
                 nc.vector.tensor_reduce(out=tops[:, g : g + 1], in_=bank[:, :, 0:width], axis=AXIS.XY, op=ALU.max)
                 banks.append(bank)
             shift = small.tile([P, 1], F32, tag="shift")
-            if spans == 1:
+            if spans_seen(a) == 1:
                 nc.vector.tensor_scalar_mul(out=shift[:], in0=tops[:, 0:1], scalar1=-SCALE)
             else:
                 nc.vector.tensor_scalar(
                     out=shift[:], in0=tops[:, 0:1], scalar1=tops[:, 1:2], scalar2=-SCALE, op0=ALU.max, op1=ALU.mult
                 )
-            for g in range(spans):
+            scored[(h, a)] = (banks, shift)
+
+        def exponentials(h, a):
+            banks, shift = scored[(h, a)]
+            for g in range(spans_seen(a)):
                 width = HALF * blocks_seen(a, g)
-                t, half = place_of(a, g)
                 nc.scalar.activation(
-                    out=e_tiles[h % 2][t][:, half, :, 0:width],
+                    out=e_tiles[h % 2][a][:, g, :, 0:width],
                     in_=banks[g][:, :, 0:width],
                     func=ACT.Exp,
                     bias=shift[:, 0:1],
                     scale=SCALE,
-                    accum_out=sums[:, g, a : a + 1],
+                    accum_out=row_sums[h][:, g, a : a + 1],
                 )
 
-        def quantise_e(h, t):
-            words = e_operands.tile([P, 2, P], U32, tag="e_words", align_bytes=64)
-            scales = e_operands.tile([P, 2, P], U8, tag="e_scales", align_bytes=64)
-            quantise_rows(e_tiles[h % 2][t][:].rearrange("p n u z -> p (n u z)"), words[:], scales[:])
-            return words, scales
+        def turn_e(h, a):
+            rows = e_tiles[h % 2][a][:].rearrange("p g u z -> p (g u z)")
+            e_grouped[(h, a)] = turn_rows(rows, spans_seen(a), nc.scalar.copy)
 
-        def attend(h, upper, e_mx, sums):
+        def quantise_e(h, a):
+            words = e_operands.tile([P, spans_seen(a), P], U32, tag="e_words", align_bytes=64)
+            scales = e_operands.tile([P, spans_seen(a), P], U8, tag="e_scales", align_bytes=64)
+            quantise(e_grouped[(h, a)], words[:], scales[:])
+            e_mx[(h, a)] = (words, scales)
+
+        def attend(h, upper):
             first = BLOCKS * upper
             product = psum_products.tile([P, BLOCKS, D], F32, tag="product")
             for j in range(BLOCKS):
+                words, scales = e_mx[(h, first + j)]
                 for g in range(upper + 1):
-                    t, half = place_of(first + j, g)
-                    words, scales = e_mx[t]
                     nc.tensor.matmul_mx(
                         out=product[:, j, :],
-                        lhsT=words[:, half, :].bitcast(FP8X4),
-                        lhsT_scale=scales[:, half, :],
+                        lhsT=words[:, g, :].bitcast(FP8X4),
+                        lhsT_scale=scales[:, g, :],
                         rhs=v_words[:, h, g, :].bitcast(FP8X4),
                         rhs_scale=v_scales[:, h, g, :],
                         start=(g == 0),
                         stop=(g == upper),
                     )
+            sums = row_sums[h]
             inverse = small.tile([P, BLOCKS], F32, tag="inverse")
             if upper == 0:
                 nc.vector.reciprocal(out=inverse[:], in_=sums[:, 0, 0:BLOCKS])
@@ -267,27 +302,31 @@ def tile_bloomattention_pa_kernel(tc, q, k, hidden_states, w_v, b_v, out):
             )
             nc.sync.dma_start(out=out_rows[:, first : first + BLOCKS, h, :], in_=result[:])
 
-        out_rows = out.rearrange("b (a p) (h d) -> p (b a) h d", p=P, d=D)
-
-        qT, kT = turn_q_and_k(0)
-        for h in range(HEADS):
-            sums = small.tile([P, SPANS, Q_TILES], F32, tag="sums")
-            e_mx = {}
-            for a in range(BLOCKS):
-                softmax_rows(h, a, qT, kT, sums)
-                if a % 2 == 1:
-                    e_mx[a // 2] = quantise_e(h, a // 2)
-            if h == 0:
-                for g in range(SPANS):
-                    for s in range(PACK):
-                        quantise_rows(hs_sb[:, g, s, :], hs_words[:, g, s], hs_scales[:, g, s])
-            quantise_rows(w_sb[:, h, :], w_words[:, h], w_scales[:, h])
-            project_v(h)
-            attend(h, 0, e_mx, sums)
-            following = turn_q_and_k(h + 1) if h + 1 < HEADS else None
-            for a in range(BLOCKS, Q_TILES):
-                softmax_rows(h, a, qT, kT, sums)
-                e_mx[a - 2] = quantise_e(h, a - 2)
-            attend(h, 1, e_mx, sums)
-            if following is not None:
-                qT, kT = following
+        tiles = [(h, a) for h in range(HEADS) for a in range(Q_TILES)]
+        turn_q_and_k(0, 0)
+        for step in range(len(tiles) + Q_TILES):
+            h, a = divmod(step, Q_TILES)
+            if h < HEADS:
+                if a == 0:
+                    row_sums[h] = small.tile([P, SPANS, Q_TILES], F32, tag="sums", name="sums_%d" % h)
+                scores(h, a)
+            if LAG_TURN <= step < len(tiles) + LAG_TURN:
+                turn_e(*tiles[step - LAG_TURN])
+            if h < HEADS:
+                exponentials(h, a)
+            if LAG_QUANTISE <= step < len(tiles) + LAG_QUANTISE:
+                quantise_e(*tiles[step - LAG_QUANTISE])
+            if a == 2 and h < HEADS:
+                turn_q_and_k(h, 1)
+            if a == 3 and h > 0:
+                attend(h - 1, 0)
+                attend(h - 1, 1)
+            if a == 6 and h + 1 < HEADS:
+                turn_q_and_k(h + 1, 0)
+            if a == 7 and h < HEADS:
+                if h == 0:
+                    quantise_hidden_states()
+                    quantise_w(0)
+                project_v(h)
+                if h + 1 < HEADS:
+                    quantise_w(h + 1)

@@ -12,7 +12,6 @@ U8 = mybir.dt.uint8
 FP8X4 = mybir.dt.float8_e4m3fn_x4
 ALU = mybir.AluOpType
 ACT = mybir.ActivationFunctionType
-AXIS = mybir.AxisListType
 
 P = 128
 PACK = 4
@@ -56,6 +55,8 @@ def tile_bloomattention_pa_kernel(tc, q, k, hidden_states, w_v, b_v, out):
         stage = ctx.enter_context(tc.tile_pool(name="stage", bufs=4))
         e_operands = ctx.enter_context(tc.tile_pool(name="e_operands", bufs=12))
         small = ctx.enter_context(tc.tile_pool(name="small", bufs=6))
+        terms = ctx.enter_context(tc.tile_pool(name="terms", bufs=3))
+        score_pool = ctx.enter_context(tc.tile_pool(name="score_pool", bufs=8))
         results = ctx.enter_context(tc.tile_pool(name="results", bufs=4))
         psum_scores = ctx.enter_context(tc.psum_pool(name="psum_scores", bufs=4))
         psum_turned = ctx.enter_context(tc.psum_pool(name="psum_turned", bufs=2))
@@ -112,14 +113,19 @@ def tile_bloomattention_pa_kernel(tc, q, k, hidden_states, w_v, b_v, out):
         nc.vector.tensor_scalar(
             out=mask[:], in0=ahead_i32[:], scalar1=0.0, scalar2=MASKED / SCALE, op0=ALU.is_lt, op1=ALU.mult
         )
-        slope_term = consts.tile([P, HEADS, Q_TILES], F32)
-        diagonal_term = consts.tile([P, HEADS, P], F32)
-        for h in range(HEADS):
+
+        added_terms = {}
+
+        def make_added_terms(h):
             slope = 0.5 ** (h + 1)
-            nc.vector.tensor_scalar_mul(out=slope_term[:, h, :], in0=position[:], scalar1=slope / SCALE)
-            nc.vector.tensor_scalar(
-                out=diagonal_term[:, h, :], in0=mask[:], scalar1=slope_term[:, h, 0:1], scalar2=None, op0=ALU.add
+            term = terms.tile([P, Q_TILES, P], F32, tag="term")
+            nc.vector.tensor_scalar_mul(
+                out=term[:], in0=position[:].unsqueeze(2).to_broadcast([P, Q_TILES, P]), scalar1=slope / SCALE
             )
+            nc.vector.tensor_tensor(out=term[:, 0, :], in0=term[:, 0, :], in1=mask[:], op=ALU.add)
+            added_terms[h] = term
+
+        make_added_terms(0)
 
         hs_words = operands.tile([P, SPANS, PACK, SPANS, P], U32, align_bytes=64)
         hs_scales = operands.tile([P, SPANS, PACK, SPANS, P], U8, align_bytes=64)
@@ -210,20 +216,16 @@ def tile_bloomattention_pa_kernel(tc, q, k, hidden_states, w_v, b_v, out):
 
         def scores(h, a):
             tops = small.tile([P, SPANS], F32, tag="tops")
-            banks = []
+            spans = []
             for g in range(spans_seen(a)):
                 blocks = blocks_seen(a, g)
                 width = HALF * blocks
                 bank = psum_scores.tile([P, 2, 2 * P], F32, tag="scores")
                 for block in range(blocks):
                     behind = a - (BLOCKS * g + block)
-                    if behind == 0:
-                        term = diagonal_term[:, h, :]
-                    else:
-                        term = slope_term[:, h, behind : behind + 1].to_broadcast([P, P])
                     nc.tensor.matmul(
                         out=bank[:, :, HALF * block : HALF * (block + 1)],
-                        lhsT=term,
+                        lhsT=added_terms[h][:, behind, :],
                         rhs=ident_f32[:].rearrange("p (u z) -> p u z", u=2),
                         is_transpose=True,
                         start=(block == 0),
@@ -236,27 +238,36 @@ def tile_bloomattention_pa_kernel(tc, q, k, hidden_states, w_v, b_v, out):
                     start=False,
                     stop=True,
                 )
-                nc.vector.tensor_reduce(out=tops[:, g : g + 1], in_=bank[:, :, 0:width], axis=AXIS.XY, op=ALU.max)
-                banks.append(bank)
+                s_sb = score_pool.tile([P, 2, 2 * P], F32, tag="s")
+                nc.vector.tensor_scalar(
+                    out=s_sb[:, :, 0:width],
+                    in0=bank[:, :, 0:width],
+                    scalar1=SCALE,
+                    scalar2=None,
+                    op0=ALU.mult,
+                    op1=ALU.max,
+                    accum_out=tops[:, g : g + 1],
+                )
+                spans.append(s_sb)
             shift = small.tile([P, 1], F32, tag="shift")
             if spans_seen(a) == 1:
-                nc.vector.tensor_scalar_mul(out=shift[:], in0=tops[:, 0:1], scalar1=-SCALE)
+                nc.vector.tensor_scalar_mul(out=shift[:], in0=tops[:, 0:1], scalar1=-1.0)
             else:
                 nc.vector.tensor_scalar(
-                    out=shift[:], in0=tops[:, 0:1], scalar1=tops[:, 1:2], scalar2=-SCALE, op0=ALU.max, op1=ALU.mult
+                    out=shift[:], in0=tops[:, 0:1], scalar1=tops[:, 1:2], scalar2=-1.0, op0=ALU.max, op1=ALU.mult
                 )
-            scored[(h, a)] = (banks, shift)
+            scored[(h, a)] = (spans, shift)
 
         def exponentials(h, a):
-            banks, shift = scored[(h, a)]
+            spans, shift = scored[(h, a)]
             for g in range(spans_seen(a)):
                 width = HALF * blocks_seen(a, g)
                 nc.scalar.activation(
                     out=e_tiles[h % 2][a][:, g, :, 0:width],
-                    in_=banks[g][:, :, 0:width],
+                    in_=spans[g][:, :, 0:width],
                     func=ACT.Exp,
                     bias=shift[:, 0:1],
-                    scale=SCALE,
+                    scale=1.0,
                     accum_out=row_sums[h][:, g, a : a + 1],
                 )
 
@@ -321,6 +332,8 @@ def tile_bloomattention_pa_kernel(tc, q, k, hidden_states, w_v, b_v, out):
             if a == 3 and h > 0:
                 attend(h - 1, 0)
                 attend(h - 1, 1)
+            if a == 5 and h + 1 < HEADS:
+                make_added_terms(h + 1)
             if a == 6 and h + 1 < HEADS:
                 turn_q_and_k(h + 1, 0)
             if a == 7 and h < HEADS:

@@ -24,12 +24,12 @@ Q_TILES = SEQ // P
 SPANS = SEQ // SPAN
 BLOCKS = SPAN // P
 HALF = P // 2
+PLANE = SPAN // 2
 
 SCALE = 1.0 / math.sqrt(D)
-MASKED = -10000.0
+MASKED = -(2.0**25)
 
 FLOPS = 2 * SEQ * HIDDEN * HIDDEN + 2 * (2 * HEADS * D * (SPAN * SPAN + SPAN * SEQ))
-
 
 LAG_TURN = 2
 LAG_QUANTISE = 3
@@ -41,6 +41,10 @@ def spans_seen(a):
 
 def blocks_seen(a, g):
     return min(a + 1 - BLOCKS * g, BLOCKS)
+
+
+def columns_seen(a):
+    return HALF * (a + 1)
 
 
 def tile_bloomattention_pa_kernel(tc, q, k, hidden_states, w_v, b_v, out):
@@ -55,8 +59,7 @@ def tile_bloomattention_pa_kernel(tc, q, k, hidden_states, w_v, b_v, out):
         stage = ctx.enter_context(tc.tile_pool(name="stage", bufs=4))
         e_operands = ctx.enter_context(tc.tile_pool(name="e_operands", bufs=12))
         small = ctx.enter_context(tc.tile_pool(name="small", bufs=6))
-        terms = ctx.enter_context(tc.tile_pool(name="terms", bufs=3))
-        score_pool = ctx.enter_context(tc.tile_pool(name="score_pool", bufs=8))
+        score_pool = ctx.enter_context(tc.tile_pool(name="score_pool", bufs=4))
         results = ctx.enter_context(tc.tile_pool(name="results", bufs=4))
         psum_scores = ctx.enter_context(tc.psum_pool(name="psum_scores", bufs=4))
         psum_turned = ctx.enter_context(tc.psum_pool(name="psum_turned", bufs=2))
@@ -70,14 +73,20 @@ def tile_bloomattention_pa_kernel(tc, q, k, hidden_states, w_v, b_v, out):
         hs_rows = hidden_states.rearrange("b (g p s) f -> p (b g) s f", p=P, s=PACK)
         w_sb = inputs.tile([P, HEADS, HIDDEN], BF16)
         w_rows = w_v.rearrange("(o p) f -> p o f", p=P)
-        nc.sync.dma_start(out=k_sb[:, 0:2], in_=k_rows[:, 0:2])
-        nc.sync.dma_start(out=q_sb[:, 0:4], in_=q_rows[:, 0:4])
-        nc.sync.dma_start(out=k_sb[:, 2:4], in_=k_rows[:, 2:4])
-        nc.sync.dma_start(out=q_sb[:, 4:8], in_=q_rows[:, 4:8])
+        early = slice(0, HIDDEN // 2)
+        late = slice(HIDDEN // 2, HIDDEN)
+        for half in range(2):
+            for c in range(2 * half, 2 * half + 2):
+                nc.sync.dma_start(out=k_sb[:, c, :, early], in_=k_rows[:, c, :, early])
+            tiles_of_half = slice(BLOCKS * half, BLOCKS * (half + 1))
+            nc.sync.dma_start(out=q_sb[:, tiles_of_half, early], in_=q_rows[:, tiles_of_half, early])
         nc.sync.dma_start(out=hs_sb[:, 0:1], in_=hs_rows[:, 0:1])
         nc.sync.dma_start(out=hs_sb[:, 1:2], in_=hs_rows[:, 1:2])
         nc.sync.dma_start(out=w_sb[:, 0:4], in_=w_rows[:, 0:4])
         nc.sync.dma_start(out=w_sb[:, 4:8], in_=w_rows[:, 4:8])
+        for c in range(2 * SPANS):
+            nc.sync.dma_start(out=k_sb[:, c, :, late], in_=k_rows[:, c, :, late])
+        nc.sync.dma_start(out=q_sb[:, :, late], in_=q_rows[:, :, late])
         bias_sb = inputs.tile([P, HIDDEN], BF16)
         nc.scalar.dma_start(out=bias_sb[:], in_=b_v.partition_broadcast(P))
         out_rows = out.rearrange("b (a p) (h d) -> p (b a) h d", p=P, d=D)
@@ -86,46 +95,58 @@ def tile_bloomattention_pa_kernel(tc, q, k, hidden_states, w_v, b_v, out):
         make_identity(nc, ident_bf[:])
         ident_f32 = consts.tile([P, P], F32)
         make_identity(nc, ident_f32[:])
-
-        position_i32 = consts.tile([P, Q_TILES], I32)
+        position_i32 = consts.tile([P, BLOCKS], I32)
         ahead_i32 = consts.tile([P, P], I32)
         for u in range(2):
             plane = slice(HALF * u, HALF * (u + 1))
             nc.gpsimd.iota(
-                position_i32[plane, :], pattern=[[-P, Q_TILES]], base=u - (P - 1), channel_multiplier=2
+                position_i32[plane, :], pattern=[[P, BLOCKS]], base=u - (SPAN - 1), channel_multiplier=2
             )
             nc.gpsimd.iota(ahead_i32[plane, :], pattern=[[1, P]], base=-u, channel_multiplier=-2)
+        earlier_i32 = consts.tile([P, 2, PLANE], I32)
+        nc.gpsimd.iota(earlier_i32[:], pattern=[[1, 2], [2, PLANE]], base=1 - 2 * SPAN, channel_multiplier=0)
+        ones_bf = consts.tile([P, P], BF16)
+        nc.gpsimd.memset(ones_bf[:], 1.0)
 
         e_tiles = []
         for parity in range(2):
             e_tiles.append([])
             for a in range(Q_TILES):
-                e_tile = e_pool.tile([P, spans_seen(a), 2, 2 * P], BF16, name="e_%d_%d" % (parity, a))
+                e_tile = e_pool.tile([P, 2, PLANE * spans_seen(a)], BF16, name="e_%d_%d" % (parity, a))
                 e_tiles[parity].append(e_tile)
-                last = spans_seen(a) - 1
-                unseen = HALF * blocks_seen(a, last)
-                if unseen < 2 * P:
-                    nc.vector.memset(e_tile[:, last, :, unseen:], 0.0)
+                if columns_seen(a) < PLANE * spans_seen(a):
+                    nc.vector.memset(e_tile[:, :, columns_seen(a) :], 0.0)
 
-        position = consts.tile([P, Q_TILES], F32)
+        position = consts.tile([P, BLOCKS], F32)
         nc.vector.tensor_copy(out=position[:], in_=position_i32[:])
         mask = consts.tile([P, P], F32)
         nc.vector.tensor_scalar(
-            out=mask[:], in0=ahead_i32[:], scalar1=0.0, scalar2=MASKED / SCALE, op0=ALU.is_lt, op1=ALU.mult
+            out=mask[:], in0=ahead_i32[:], scalar1=0.0, scalar2=MASKED, op0=ALU.is_lt, op1=ALU.mult
+        )
+        added_terms = consts.tile([P, 2, BLOCKS, P], F32)
+        nc.vector.tensor_scalar_mul(
+            out=added_terms[:, 0], in0=position[:].unsqueeze(2).to_broadcast([P, BLOCKS, P]), scalar1=1.0 / SCALE
+        )
+        nc.vector.tensor_tensor(
+            out=added_terms[:, 1],
+            in0=added_terms[:, 0],
+            in1=mask[:].unsqueeze(1).to_broadcast([P, BLOCKS, P]),
+            op=ALU.add,
         )
 
-        added_terms = {}
-
-        def make_added_terms(h):
-            slope = 0.5 ** (h + 1)
-            term = terms.tile([P, Q_TILES, P], F32, tag="term")
-            nc.vector.tensor_scalar_mul(
-                out=term[:], in0=position[:].unsqueeze(2).to_broadcast([P, Q_TILES, P]), scalar1=slope / SCALE
-            )
-            nc.vector.tensor_tensor(out=term[:, 0, :], in0=term[:, 0, :], in1=mask[:], op=ALU.add)
-            added_terms[h] = term
-
-        make_added_terms(0)
+        earlier_rows = consts.tile([P, SPAN], BF16)
+        nc.vector.memset(earlier_rows[:], 0.0)
+        rest = consts.tile([P, SPAN], F32, name="rest_0")
+        nc.vector.tensor_scalar_mul(out=rest[:], in0=earlier_i32[:].rearrange("p u z -> p (u z)"), scalar1=1.0 / SCALE)
+        for part in range(3):
+            row = slice(32 * part, 32 * part + 1)
+            rounded = consts.tile([P, SPAN], BF16, name="rounded_%d" % part)
+            nc.vector.tensor_copy(out=rounded[:], in_=rest[:])
+            nc.vector.tensor_copy(out=earlier_rows[row, :], in_=rounded[row, :])
+            if part < 2:
+                left = consts.tile([P, SPAN], F32, name="rest_%d" % (part + 1))
+                nc.vector.tensor_sub(out=left[:], in0=rest[:], in1=rounded[:])
+                rest = left
 
         hs_words = operands.tile([P, SPANS, PACK, SPANS, P], U32, align_bytes=64)
         hs_scales = operands.tile([P, SPANS, PACK, SPANS, P], U8, align_bytes=64)
@@ -134,13 +155,12 @@ def tile_bloomattention_pa_kernel(tc, q, k, hidden_states, w_v, b_v, out):
         v_words = operands.tile([P, HEADS, SPANS, D], U32, align_bytes=64)
         v_scales = operands.tile([P, HEADS, SPANS, D], U8, align_bytes=64)
 
-        def turn_rows(rows, count, copy_out):
-            pairs = rows.bitcast(F32)
+        def turn_rows(pairs, copy_out):
+            count = pairs.shape[1]
             turned = psum_turned.tile([P, count, 2, P], F32, tag="turned")
             for c in range(count):
                 for u in range(2):
-                    first = (2 * c + u) * P
-                    nc.tensor.transpose(turned[:, c, u, :], pairs[:, first : first + P], ident_f32[:])
+                    nc.tensor.transpose(turned[:, c, u, :], pairs[:, c, u, :], ident_f32[:])
             grouped = stage.tile([P, count, P, PACK], BF16, tag="grouped", align_bytes=64)
             copy_out(out=grouped[:].bitcast(F32), in_=turned[:].rearrange("p c u r -> p c r u"))
             return grouped
@@ -152,14 +172,17 @@ def tile_bloomattention_pa_kernel(tc, q, k, hidden_states, w_v, b_v, out):
                 in_=grouped[:].rearrange("p c r s -> p (c r s)"),
             )
 
+        def feature_pairs(rows):
+            return rows.bitcast(F32).rearrange("p (c u w) -> p c u w", c=SPANS, u=2)
+
         def quantise_w(h):
-            quantise(turn_rows(w_sb[:, h, :], SPANS, nc.scalar.copy), w_words[:, h], w_scales[:, h])
+            quantise(turn_rows(feature_pairs(w_sb[:, h, :]), nc.scalar.copy), w_words[:, h], w_scales[:, h])
 
         def quantise_hidden_states():
             for g in range(SPANS):
                 for s in range(PACK):
                     copy_out = nc.scalar.copy if s % 2 == 0 else nc.vector.tensor_copy
-                    grouped = turn_rows(hs_sb[:, g, s, :], SPANS, copy_out)
+                    grouped = turn_rows(feature_pairs(hs_sb[:, g, s, :]), copy_out)
                     quantise(grouped, hs_words[:, g, s], hs_scales[:, g, s])
 
         qk_turned = {}
@@ -168,20 +191,13 @@ def tile_bloomattention_pa_kernel(tc, q, k, hidden_states, w_v, b_v, out):
             head = slice(h * D, (h + 1) * D)
             turned = psum_turned.tile([P, 2, BLOCKS, P], BF16, tag="turned")
             for j in range(BLOCKS):
-                nc.tensor.matmul(
-                    out=turned[:, 0, j, :], lhsT=q_sb[:, BLOCKS * half + j, head], rhs=ident_bf[:], start=True, stop=True
-                )
+                nc.tensor.transpose(turned[:, 0, j, :], q_sb[:, BLOCKS * half + j, head], ident_bf[:])
             for u in range(2):
                 for f in range(2):
-                    nc.tensor.matmul(
-                        out=turned[:, 1, 2 * u + f, :],
-                        lhsT=k_sb[:, 2 * half + f, u, head],
-                        rhs=ident_bf[:],
-                        start=True,
-                        stop=True,
-                    )
+                    nc.tensor.transpose(turned[:, 1, 2 * u + f, :], k_sb[:, 2 * half + f, u, head], ident_bf[:])
             qk = turned_heads.tile([P, 2, BLOCKS, P], BF16, tag="qk")
-            nc.scalar.copy(out=qk[:], in_=turned[:])
+            nc.scalar.mul(out=qk[:, 0], in_=turned[:, 0], mul=2.0 ** (h + 1))
+            nc.scalar.copy(out=qk[:, 1], in_=turned[:, 1])
             qk_turned[(h, half)] = qk
 
         def project_v(h):
@@ -215,22 +231,31 @@ def tile_bloomattention_pa_kernel(tc, q, k, hidden_states, w_v, b_v, out):
         e_mx = {}
 
         def scores(h, a):
-            tops = small.tile([P, SPANS], F32, tag="tops")
-            spans = []
+            minus_s = score_pool.tile([P, 2, PLANE * spans_seen(a)], F32, tag="minus_s")
+            lows = small.tile([P, SPANS], F32, tag="lows")
             for g in range(spans_seen(a)):
                 blocks = blocks_seen(a, g)
                 width = HALF * blocks
-                bank = psum_scores.tile([P, 2, 2 * P], F32, tag="scores")
-                for block in range(blocks):
-                    behind = a - (BLOCKS * g + block)
+                bank = psum_scores.tile([P, 2, PLANE], F32, tag="scores")
+                if g < a // BLOCKS:
                     nc.tensor.matmul(
-                        out=bank[:, :, HALF * block : HALF * (block + 1)],
-                        lhsT=added_terms[h][:, behind, :],
-                        rhs=ident_f32[:].rearrange("p (u z) -> p u z", u=2),
-                        is_transpose=True,
-                        start=(block == 0),
+                        out=bank[:].rearrange("p u z -> p (u z)"),
+                        lhsT=ones_bf[:],
+                        rhs=earlier_rows[:],
+                        start=True,
                         stop=False,
                     )
+                else:
+                    for block in range(blocks):
+                        masked = 1 if block == a % BLOCKS else 0
+                        nc.tensor.matmul(
+                            out=bank[:, :, HALF * block : HALF * (block + 1)],
+                            lhsT=added_terms[:, masked, block, :],
+                            rhs=ident_f32[:].rearrange("p (u z) -> p u z", u=2),
+                            is_transpose=True,
+                            start=(block == 0),
+                            stop=False,
+                        )
                 nc.tensor.matmul(
                     out=bank[:, :, 0:width],
                     lhsT=qk_turned[(h, a // BLOCKS)][:, 0, a % BLOCKS, :],
@@ -238,42 +263,36 @@ def tile_bloomattention_pa_kernel(tc, q, k, hidden_states, w_v, b_v, out):
                     start=False,
                     stop=True,
                 )
-                s_sb = score_pool.tile([P, 2, 2 * P], F32, tag="s")
                 nc.vector.tensor_scalar(
-                    out=s_sb[:, :, 0:width],
+                    out=minus_s[:, :, PLANE * g : PLANE * g + width],
                     in0=bank[:, :, 0:width],
-                    scalar1=SCALE,
+                    scalar1=-SCALE * 0.5 ** (h + 1),
                     scalar2=None,
                     op0=ALU.mult,
-                    op1=ALU.max,
-                    accum_out=tops[:, g : g + 1],
+                    op1=ALU.min,
+                    accum_out=lows[:, g : g + 1],
                 )
-                spans.append(s_sb)
-            shift = small.tile([P, 1], F32, tag="shift")
             if spans_seen(a) == 1:
-                nc.vector.tensor_scalar_mul(out=shift[:], in0=tops[:, 0:1], scalar1=-1.0)
+                scored[(h, a)] = (minus_s, lows)
             else:
-                nc.vector.tensor_scalar(
-                    out=shift[:], in0=tops[:, 0:1], scalar1=tops[:, 1:2], scalar2=-1.0, op0=ALU.max, op1=ALU.mult
-                )
-            scored[(h, a)] = (spans, shift)
+                lowest = small.tile([P, 1], F32, tag="lowest")
+                nc.vector.tensor_tensor(out=lowest[:], in0=lows[:, 0:1], in1=lows[:, 1:2], op=ALU.min)
+                scored[(h, a)] = (minus_s, lowest)
 
         def exponentials(h, a):
-            spans, shift = scored[(h, a)]
-            for g in range(spans_seen(a)):
-                width = HALF * blocks_seen(a, g)
-                nc.scalar.activation(
-                    out=e_tiles[h % 2][a][:, g, :, 0:width],
-                    in_=spans[g][:, :, 0:width],
-                    func=ACT.Exp,
-                    bias=shift[:, 0:1],
-                    scale=1.0,
-                    accum_out=row_sums[h][:, g, a : a + 1],
-                )
+            minus_s, minus_top = scored[(h, a)]
+            nc.scalar.activation(
+                out=e_tiles[h % 2][a][:, :, 0 : columns_seen(a)],
+                in_=minus_s[:, :, 0 : columns_seen(a)],
+                func=ACT.Exp,
+                bias=minus_top[:, 0:1],
+                scale=-1.0,
+                accum_out=row_sums[h][:, a : a + 1],
+            )
 
         def turn_e(h, a):
-            rows = e_tiles[h % 2][a][:].rearrange("p g u z -> p (g u z)")
-            e_grouped[(h, a)] = turn_rows(rows, spans_seen(a), nc.scalar.copy)
+            pairs = e_tiles[h % 2][a][:].bitcast(F32).rearrange("p u (g w) -> p g u w", w=P)
+            e_grouped[(h, a)] = turn_rows(pairs, nc.scalar.copy)
 
         def quantise_e(h, a):
             words = e_operands.tile([P, spans_seen(a), P], U32, tag="e_words", align_bytes=64)
@@ -296,14 +315,8 @@ def tile_bloomattention_pa_kernel(tc, q, k, hidden_states, w_v, b_v, out):
                         start=(g == 0),
                         stop=(g == upper),
                     )
-            sums = row_sums[h]
             inverse = small.tile([P, BLOCKS], F32, tag="inverse")
-            if upper == 0:
-                nc.vector.reciprocal(out=inverse[:], in_=sums[:, 0, 0:BLOCKS])
-            else:
-                total = small.tile([P, BLOCKS], F32, tag="total")
-                nc.vector.tensor_tensor(out=total[:], in0=sums[:, 0, first:], in1=sums[:, 1, first:], op=ALU.add)
-                nc.vector.reciprocal(out=inverse[:], in_=total[:])
+            nc.vector.reciprocal(out=inverse[:], in_=row_sums[h][:, first : first + BLOCKS])
             result = results.tile([P, BLOCKS, D], F32, tag="result")
             nc.vector.tensor_tensor(
                 out=result[:],
@@ -319,7 +332,7 @@ def tile_bloomattention_pa_kernel(tc, q, k, hidden_states, w_v, b_v, out):
             h, a = divmod(step, Q_TILES)
             if h < HEADS:
                 if a == 0:
-                    row_sums[h] = small.tile([P, SPANS, Q_TILES], F32, tag="sums", name="sums_%d" % h)
+                    row_sums[h] = small.tile([P, Q_TILES], F32, tag="sums", name="sums_%d" % h)
                 scores(h, a)
             if LAG_TURN <= step < len(tiles) + LAG_TURN:
                 turn_e(*tiles[step - LAG_TURN])
@@ -332,8 +345,6 @@ def tile_bloomattention_pa_kernel(tc, q, k, hidden_states, w_v, b_v, out):
             if a == 3 and h > 0:
                 attend(h - 1, 0)
                 attend(h - 1, 1)
-            if a == 5 and h + 1 < HEADS:
-                make_added_terms(h + 1)
             if a == 6 and h + 1 < HEADS:
                 turn_q_and_k(h + 1, 0)
             if a == 7 and h < HEADS:

@@ -61,8 +61,8 @@ def tile_bloomattention_pa_kernel(tc, q, k, hidden_states, w_v, b_v, out):
         small = ctx.enter_context(tc.tile_pool(name="small", bufs=6))
         score_pool = ctx.enter_context(tc.tile_pool(name="score_pool", bufs=4))
         results = ctx.enter_context(tc.tile_pool(name="results", bufs=4))
-        psum_scores = ctx.enter_context(tc.psum_pool(name="psum_scores", bufs=4))
-        psum_turned = ctx.enter_context(tc.psum_pool(name="psum_turned", bufs=2))
+        psum_scores = ctx.enter_context(tc.psum_pool(name="psum_scores", bufs=3))
+        psum_turned = ctx.enter_context(tc.psum_pool(name="psum_turned", bufs=3))
         psum_products = ctx.enter_context(tc.psum_pool(name="psum_products", bufs=2))
 
         k_sb = inputs.tile([P, 2 * SPANS, 2, HIDDEN], BF16)
@@ -340,12 +340,12 @@ def tile_bloomattention_pa_kernel(tc, q, k, hidden_states, w_v, b_v, out):
                 exponentials(h, a)
             if LAG_QUANTISE <= step < len(tiles) + LAG_QUANTISE:
                 quantise_e(*tiles[step - LAG_QUANTISE])
-            if a == 2 and h < HEADS:
+            if a == 1 and h < HEADS:
                 turn_q_and_k(h, 1)
             if a == 3 and h > 0:
                 attend(h - 1, 0)
                 attend(h - 1, 1)
-            if a == 6 and h + 1 < HEADS:
+            if a == 4 and h + 1 < HEADS:
                 turn_q_and_k(h + 1, 0)
             if a == 7 and h < HEADS:
                 if h == 0:

@@ -175,8 +175,13 @@ def tile_bloomattention_pa_kernel(tc, q, k, hidden_states, w_v, b_v, out):
         def feature_pairs(rows):
             return rows.bitcast(F32).rearrange("p (c u w) -> p c u w", c=SPANS, u=2)
 
+        w_grouped = {}
+
+        def turn_w(h):
+            w_grouped[h] = turn_rows(feature_pairs(w_sb[:, h, :]), nc.scalar.copy)
+
         def quantise_w(h):
-            quantise(turn_rows(feature_pairs(w_sb[:, h, :]), nc.scalar.copy), w_words[:, h], w_scales[:, h])
+            quantise(w_grouped[h], w_words[:, h], w_scales[:, h])
 
         def quantise_hidden_states():
             for g in range(SPANS):
@@ -191,7 +196,11 @@ def tile_bloomattention_pa_kernel(tc, q, k, hidden_states, w_v, b_v, out):
             head = slice(h * D, (h + 1) * D)
             turned = psum_turned.tile([P, 2, BLOCKS, P], BF16, tag="turned")
             for j in range(BLOCKS):
-                nc.tensor.transpose(turned[:, 0, j, :], q_sb[:, BLOCKS * half + j, head], ident_bf[:])
+                q_block = q_sb[:, BLOCKS * half + j, head]
+                if half == 1:
+                    nc.tensor.matmul(out=turned[:, 0, j, :], lhsT=q_block, rhs=ident_bf[:], start=True, stop=True)
+                else:
+                    nc.tensor.transpose(turned[:, 0, j, :], q_block, ident_bf[:])
             for u in range(2):
                 for f in range(2):
                     nc.tensor.transpose(turned[:, 1, 2 * u + f, :], k_sb[:, 2 * half + f, u, head], ident_bf[:])
@@ -340,6 +349,8 @@ def tile_bloomattention_pa_kernel(tc, q, k, hidden_states, w_v, b_v, out):
                 exponentials(h, a)
             if LAG_QUANTISE <= step < len(tiles) + LAG_QUANTISE:
                 quantise_e(*tiles[step - LAG_QUANTISE])
+            if a == 1 and 0 < h < HEADS:
+                quantise_w(h)
             if a == 1 and h < HEADS:
                 turn_q_and_k(h, 1)
             if a == 3 and h > 0:
@@ -350,7 +361,8 @@ def tile_bloomattention_pa_kernel(tc, q, k, hidden_states, w_v, b_v, out):
             if a == 7 and h < HEADS:
                 if h == 0:
                     quantise_hidden_states()
+                    turn_w(0)
                     quantise_w(0)
                 project_v(h)
                 if h + 1 < HEADS:
-                    quantise_w(h + 1)
+                    turn_w(h + 1)

@@ -56,7 +56,7 @@ def tile_bloomattention_pa_kernel(tc, q, k, hidden_states, w_v, b_v, out):
         operands = ctx.enter_context(tc.tile_pool(name="operands", bufs=1))
         e_pool = ctx.enter_context(tc.tile_pool(name="e_pool", bufs=1))
         turned_heads = ctx.enter_context(tc.tile_pool(name="turned_heads", bufs=4))
-        stage = ctx.enter_context(tc.tile_pool(name="stage", bufs=4))
+        stage = ctx.enter_context(tc.tile_pool(name="stage", bufs=6))
         e_operands = ctx.enter_context(tc.tile_pool(name="e_operands", bufs=12))
         small = ctx.enter_context(tc.tile_pool(name="small", bufs=6))
         score_pool = ctx.enter_context(tc.tile_pool(name="score_pool", bufs=4))
@@ -184,11 +184,17 @@ def tile_bloomattention_pa_kernel(tc, q, k, hidden_states, w_v, b_v, out):
             quantise(w_grouped[h], w_words[:, h], w_scales[:, h])
 
         def quantise_hidden_states():
-            for g in range(SPANS):
-                for s in range(PACK):
-                    copy_out = nc.scalar.copy if s % 2 == 0 else nc.vector.tensor_copy
-                    grouped = turn_rows(feature_pairs(hs_sb[:, g, s, :]), copy_out)
-                    quantise(grouped, hs_words[:, g, s], hs_scales[:, g, s])
+            pieces = [(g, s) for g in range(SPANS) for s in range(PACK)]
+            waiting = []
+            for g, s in pieces:
+                copy_out = nc.scalar.copy if s % 2 == 0 else nc.vector.tensor_copy
+                waiting.append((turn_rows(feature_pairs(hs_sb[:, g, s, :]), copy_out), g, s))
+                if len(waiting) > 1:
+                    grouped, g0, s0 = waiting[0]
+                    waiting = waiting[1:]
+                    quantise(grouped, hs_words[:, g0, s0], hs_scales[:, g0, s0])
+            grouped, g0, s0 = waiting[0]
+            quantise(grouped, hs_words[:, g0, s0], hs_scales[:, g0, s0])
 
         qk_turned = {}
 
@@ -232,8 +238,13 @@ def tile_bloomattention_pa_kernel(tc, q, k, hidden_states, w_v, b_v, out):
                     in1=bias_sb[:, head].unsqueeze(2).to_broadcast([P, D, PACK]),
                     op=ALU.add,
                 )
-            quantise(grouped, v_words[:, h], v_scales[:, h])
+            v_grouped[h] = grouped
 
+        def quantise_v(h):
+            quantise(v_grouped[h], v_words[:, h], v_scales[:, h])
+
+        v_grouped = {}
+        inverses = {}
         row_sums = {}
         scored = {}
         e_grouped = {}
@@ -281,9 +292,11 @@ def tile_bloomattention_pa_kernel(tc, q, k, hidden_states, w_v, b_v, out):
                     op1=ALU.min,
                     accum_out=lows[:, g : g + 1],
                 )
-            if spans_seen(a) == 1:
-                scored[(h, a)] = (minus_s, lows)
-            else:
+            scored[(h, a)] = (minus_s, lows)
+
+        def join_lows(h, a):
+            if spans_seen(a) == 2:
+                minus_s, lows = scored[(h, a)]
                 lowest = small.tile([P, 1], F32, tag="lowest")
                 nc.vector.tensor_tensor(out=lowest[:], in0=lows[:, 0:1], in1=lows[:, 1:2], op=ALU.min)
                 scored[(h, a)] = (minus_s, lowest)
@@ -324,13 +337,11 @@ def tile_bloomattention_pa_kernel(tc, q, k, hidden_states, w_v, b_v, out):
                         start=(g == 0),
                         stop=(g == upper),
                     )
-            inverse = small.tile([P, BLOCKS], F32, tag="inverse")
-            nc.vector.reciprocal(out=inverse[:], in_=row_sums[h][:, first : first + BLOCKS])
             result = results.tile([P, BLOCKS, D], F32, tag="result")
             nc.vector.tensor_tensor(
                 out=result[:],
                 in0=product[:],
-                in1=inverse[:].unsqueeze(2).to_broadcast([P, BLOCKS, D]),
+                in1=inverses[h][:, first : first + BLOCKS].unsqueeze(2).to_broadcast([P, BLOCKS, D]),
                 op=ALU.mult,
             )
             nc.sync.dma_start(out=out_rows[:, first : first + BLOCKS, h, :], in_=result[:])
@@ -343,12 +354,18 @@ def tile_bloomattention_pa_kernel(tc, q, k, hidden_states, w_v, b_v, out):
                 if a == 0:
                     row_sums[h] = small.tile([P, Q_TILES], F32, tag="sums", name="sums_%d" % h)
                 scores(h, a)
+            if a == 0 and 0 < h <= HEADS:
+                quantise_v(h - 1)
             if LAG_TURN <= step < len(tiles) + LAG_TURN:
                 turn_e(*tiles[step - LAG_TURN])
-            if h < HEADS:
-                exponentials(h, a)
             if LAG_QUANTISE <= step < len(tiles) + LAG_QUANTISE:
                 quantise_e(*tiles[step - LAG_QUANTISE])
+            if h < HEADS:
+                join_lows(h, a)
+                exponentials(h, a)
+            if a == 1 and h > 0:
+                inverses[h - 1] = small.tile([P, Q_TILES], F32, tag="inverse", name="inverse_%d" % (h - 1))
+                nc.vector.reciprocal(out=inverses[h - 1][:], in_=row_sums[h - 1][:])
             if a == 1 and 0 < h < HEADS:
                 quantise_w(h)
             if a == 1 and h < HEADS:

@@ -32,6 +32,7 @@ MASKED = -(2.0**25)
 FLOPS = 2 * SEQ * HIDDEN * HIDDEN + 2 * (2 * HEADS * D * (SPAN * SPAN + SPAN * SEQ))
 
 LAG_TURN = 2
+HS_STEP = 2
 LAG_QUANTISE = 3
 
 
@@ -57,7 +58,7 @@ def tile_bloomattention_pa_kernel(tc, q, k, hidden_states, w_v, b_v, out):
         e_pool = ctx.enter_context(tc.tile_pool(name="e_pool", bufs=1))
         turned_heads = ctx.enter_context(tc.tile_pool(name="turned_heads", bufs=4))
         stage = ctx.enter_context(tc.tile_pool(name="stage", bufs=6))
-        e_operands = ctx.enter_context(tc.tile_pool(name="e_operands", bufs=12))
+        e_operands = ctx.enter_context(tc.tile_pool(name="e_operands", bufs=16))
         small = ctx.enter_context(tc.tile_pool(name="small", bufs=6))
         score_pool = ctx.enter_context(tc.tile_pool(name="score_pool", bufs=4))
         results = ctx.enter_context(tc.tile_pool(name="results", bufs=4))
@@ -73,8 +74,9 @@ def tile_bloomattention_pa_kernel(tc, q, k, hidden_states, w_v, b_v, out):
         hs_rows = hidden_states.rearrange("b (g p s) f -> p (b g) s f", p=P, s=PACK)
         w_sb = inputs.tile([P, HEADS, HIDDEN], BF16)
         w_rows = w_v.rearrange("(o p) f -> p o f", p=P)
-        early = slice(0, HIDDEN // 2)
-        late = slice(HIDDEN // 2, HIDDEN)
+        early = slice(0, 2 * D)
+        middle = slice(2 * D, 4 * D)
+        late = slice(4 * D, HIDDEN)
         for half in range(2):
             for c in range(2 * half, 2 * half + 2):
                 nc.sync.dma_start(out=k_sb[:, c, :, early], in_=k_rows[:, c, :, early])
@@ -84,9 +86,10 @@ def tile_bloomattention_pa_kernel(tc, q, k, hidden_states, w_v, b_v, out):
         nc.sync.dma_start(out=hs_sb[:, 1:2], in_=hs_rows[:, 1:2])
         nc.sync.dma_start(out=w_sb[:, 0:4], in_=w_rows[:, 0:4])
         nc.sync.dma_start(out=w_sb[:, 4:8], in_=w_rows[:, 4:8])
-        for c in range(2 * SPANS):
-            nc.sync.dma_start(out=k_sb[:, c, :, late], in_=k_rows[:, c, :, late])
-        nc.sync.dma_start(out=q_sb[:, :, late], in_=q_rows[:, :, late])
+        for heads in (middle, late):
+            for c in range(2 * SPANS):
+                nc.sync.dma_start(out=k_sb[:, c, :, heads], in_=k_rows[:, c, :, heads])
+            nc.sync.dma_start(out=q_sb[:, :, heads], in_=q_rows[:, :, heads])
         bias_sb = inputs.tile([P, HIDDEN], BF16)
         nc.scalar.dma_start(out=bias_sb[:], in_=b_v.partition_broadcast(P))
         out_rows = out.rearrange("b (a p) (h d) -> p (b a) h d", p=P, d=D)
@@ -119,6 +122,8 @@ def tile_bloomattention_pa_kernel(tc, q, k, hidden_states, w_v, b_v, out):
 
         position = consts.tile([P, BLOCKS], F32)
         nc.vector.tensor_copy(out=position[:], in_=position_i32[:])
+        earlier = consts.tile([P, SPAN], F32)
+        nc.vector.tensor_copy(out=earlier[:], in_=earlier_i32[:].rearrange("p u z -> p (u z)"))
         mask = consts.tile([P, P], F32)
         nc.vector.tensor_scalar(
             out=mask[:], in0=ahead_i32[:], scalar1=0.0, scalar2=MASKED, op0=ALU.is_lt, op1=ALU.mult
@@ -134,19 +139,22 @@ def tile_bloomattention_pa_kernel(tc, q, k, hidden_states, w_v, b_v, out):
             op=ALU.add,
         )
 
+        def on_gpsimd(result, source, factor):
+            nc.gpsimd.tensor_scalar(out=result, in0=source, scalar1=factor, scalar2=0.0, op0=ALU.mult, op1=ALU.add)
+
         earlier_rows = consts.tile([P, SPAN], BF16)
-        nc.vector.memset(earlier_rows[:], 0.0)
+        nc.gpsimd.memset(earlier_rows[:], 0.0)
         rest = consts.tile([P, SPAN], F32, name="rest_0")
-        nc.vector.tensor_scalar_mul(out=rest[:], in0=earlier_i32[:].rearrange("p u z -> p (u z)"), scalar1=1.0 / SCALE)
+        on_gpsimd(rest[:], earlier[:], 1.0 / SCALE)
         for part in range(3):
             row = slice(32 * part, 32 * part + 1)
-            rounded = consts.tile([P, SPAN], BF16, name="rounded_%d" % part)
-            nc.vector.tensor_copy(out=rounded[:], in_=rest[:])
-            nc.vector.tensor_copy(out=earlier_rows[row, :], in_=rounded[row, :])
+            exact = rest
             if part < 2:
-                left = consts.tile([P, SPAN], F32, name="rest_%d" % (part + 1))
-                nc.vector.tensor_sub(out=left[:], in0=rest[:], in1=rounded[:])
-                rest = left
+                rounded = consts.tile([P, SPAN], BF16, name="rounded_%d" % part)
+                on_gpsimd(rounded[:], exact[:], 1.0)
+                rest = consts.tile([P, SPAN], F32, name="rest_%d" % (part + 1))
+                nc.gpsimd.tensor_tensor(out=rest[:], in0=exact[:], in1=rounded[:], op=ALU.subtract)
+            on_gpsimd(earlier_rows[row, :], exact[row, :], 1.0)
 
         hs_words = operands.tile([P, SPANS, PACK, SPANS, P], U32, align_bytes=64)
         hs_scales = operands.tile([P, SPANS, PACK, SPANS, P], U8, align_bytes=64)
@@ -183,18 +191,16 @@ def tile_bloomattention_pa_kernel(tc, q, k, hidden_states, w_v, b_v, out):
         def quantise_w(h):
             quantise(w_grouped[h], w_words[:, h], w_scales[:, h])
 
-        def quantise_hidden_states():
-            pieces = [(g, s) for g in range(SPANS) for s in range(PACK)]
-            waiting = []
-            for g, s in pieces:
-                copy_out = nc.scalar.copy if s % 2 == 0 else nc.vector.tensor_copy
-                waiting.append((turn_rows(feature_pairs(hs_sb[:, g, s, :]), copy_out), g, s))
-                if len(waiting) > 1:
-                    grouped, g0, s0 = waiting[0]
-                    waiting = waiting[1:]
-                    quantise(grouped, hs_words[:, g0, s0], hs_scales[:, g0, s0])
-            grouped, g0, s0 = waiting[0]
-            quantise(grouped, hs_words[:, g0, s0], hs_scales[:, g0, s0])
+        hs_grouped = {}
+
+        def turn_hidden_states(piece):
+            g, s = divmod(piece, PACK)
+            copy_out = nc.vector.tensor_copy if s % 2 == 0 else nc.scalar.copy
+            hs_grouped[piece] = turn_rows(feature_pairs(hs_sb[:, g, s, :]), copy_out)
+
+        def quantise_hidden_states(piece):
+            g, s = divmod(piece, PACK)
+            quantise(hs_grouped[piece], hs_words[:, g, s], hs_scales[:, g, s])
 
         qk_turned = {}
 
@@ -207,12 +213,16 @@ def tile_bloomattention_pa_kernel(tc, q, k, hidden_states, w_v, b_v, out):
                     nc.tensor.matmul(out=turned[:, 0, j, :], lhsT=q_block, rhs=ident_bf[:], start=True, stop=True)
                 else:
                     nc.tensor.transpose(turned[:, 0, j, :], q_block, ident_bf[:])
+            q_turned = turned[:, 0]
+            if (h, half) == (0, 0):
+                turned = psum_turned.tile([P, 2, BLOCKS, P], BF16, tag="turned")
             for u in range(2):
                 for f in range(2):
                     nc.tensor.transpose(turned[:, 1, 2 * u + f, :], k_sb[:, 2 * half + f, u, head], ident_bf[:])
             qk = turned_heads.tile([P, 2, BLOCKS, P], BF16, tag="qk")
-            nc.scalar.mul(out=qk[:, 0], in_=turned[:, 0], mul=2.0 ** (h + 1))
-            nc.scalar.copy(out=qk[:, 1], in_=turned[:, 1])
+            nc.scalar.mul(out=qk[:, 0], in_=q_turned, mul=2.0 ** (h + 1))
+            copy_k = nc.vector.tensor_copy if (h, half) == (0, 0) else nc.scalar.copy
+            copy_k(out=qk[:, 1], in_=turned[:, 1])
             qk_turned[(h, half)] = qk
 
         def project_v(h):
@@ -322,10 +332,15 @@ def tile_bloomattention_pa_kernel(tc, q, k, hidden_states, w_v, b_v, out):
             quantise(e_grouped[(h, a)], words[:], scales[:])
             e_mx[(h, a)] = (words, scales)
 
-        def attend(h, upper):
-            first = BLOCKS * upper
+        def invert_sums(h, first, count):
+            inverse = small.tile([P, Q_TILES], F32, tag="inverse")
+            nc.vector.reciprocal(out=inverse[:, 0:count], in_=row_sums[h][:, first : first + count])
+            inverses[(h, first)] = inverse
+
+        def attend(h, first, count):
+            upper = first // BLOCKS
             product = psum_products.tile([P, BLOCKS, D], F32, tag="product")
-            for j in range(BLOCKS):
+            for j in range(count):
                 words, scales = e_mx[(h, first + j)]
                 for g in range(upper + 1):
                     nc.tensor.matmul_mx(
@@ -339,47 +354,59 @@ def tile_bloomattention_pa_kernel(tc, q, k, hidden_states, w_v, b_v, out):
                     )
             result = results.tile([P, BLOCKS, D], F32, tag="result")
             nc.vector.tensor_tensor(
-                out=result[:],
-                in0=product[:],
-                in1=inverses[h][:, first : first + BLOCKS].unsqueeze(2).to_broadcast([P, BLOCKS, D]),
+                out=result[:, 0:count],
+                in0=product[:, 0:count],
+                in1=inverses[(h, first)][:, 0:count].unsqueeze(2).to_broadcast([P, count, D]),
                 op=ALU.mult,
             )
-            nc.sync.dma_start(out=out_rows[:, first : first + BLOCKS, h, :], in_=result[:])
+            nc.sync.dma_start(out=out_rows[:, first : first + count, h, :], in_=result[:, 0:count])
 
-        tiles = [(h, a) for h in range(HEADS) for a in range(Q_TILES)]
+        last = HEADS - 1
+        tiles = [(h, a) for h in range(last) for a in range(Q_TILES)]
+        tiles = tiles + [(last, a) for a in (4, 5, 6, 7, 3, 2, 1, 0)]
+        turned_w = {max(Q_TILES * h - 1, HS_STEP + 6 + h): h for h in range(HEADS)}
+        projected = {max(Q_TILES * h + 7, HS_STEP + 9): h for h in range(last)}
+        projected[Q_TILES * last + 4] = last
+        attended = {Q_TILES * (h + 1) + 5: [(h, 0, BLOCKS), (h, BLOCKS, BLOCKS)] for h in range(last)}
+        attended[Q_TILES * last + 7] = [(last, BLOCKS, BLOCKS)]
+        attended[Q_TILES * last + 8] = [(last, 2, 2)]
+        attended[Q_TILES * last + 10] = [(last, 0, 2)]
+
         turn_q_and_k(0, 0)
         for step in range(len(tiles) + Q_TILES):
-            h, a = divmod(step, Q_TILES)
-            if h < HEADS:
-                if a == 0:
+            head, turn = divmod(step, Q_TILES)
+            if step < len(tiles):
+                h, a = tiles[step]
+                if turn == 0:
                     row_sums[h] = small.tile([P, Q_TILES], F32, tag="sums", name="sums_%d" % h)
                 scores(h, a)
-            if a == 0 and 0 < h <= HEADS:
-                quantise_v(h - 1)
+            if step - 1 in projected:
+                quantise_v(projected[step - 1])
             if LAG_TURN <= step < len(tiles) + LAG_TURN:
                 turn_e(*tiles[step - LAG_TURN])
+            piece = step - HS_STEP
+            if 0 <= piece < SPANS * PACK:
+                turn_hidden_states(piece)
             if LAG_QUANTISE <= step < len(tiles) + LAG_QUANTISE:
                 quantise_e(*tiles[step - LAG_QUANTISE])
-            if h < HEADS:
+            if 0 <= piece - 1 < SPANS * PACK:
+                quantise_hidden_states(piece - 1)
+            if step < len(tiles):
                 join_lows(h, a)
                 exponentials(h, a)
-            if a == 1 and h > 0:
-                inverses[h - 1] = small.tile([P, Q_TILES], F32, tag="inverse", name="inverse_%d" % (h - 1))
-                nc.vector.reciprocal(out=inverses[h - 1][:], in_=row_sums[h - 1][:])
-            if a == 1 and 0 < h < HEADS:
-                quantise_w(h)
-            if a == 1 and h < HEADS:
-                turn_q_and_k(h, 1)
-            if a == 3 and h > 0:
-                attend(h - 1, 0)
-                attend(h - 1, 1)
-            if a == 4 and h + 1 < HEADS:
-                turn_q_and_k(h + 1, 0)
-            if a == 7 and h < HEADS:
-                if h == 0:
-                    quantise_hidden_states()
-                    turn_w(0)
-                    quantise_w(0)
-                project_v(h)
-                if h + 1 < HEADS:
-                    turn_w(h + 1)
+            if step - 2 in turned_w:
+                quantise_w(turned_w[step - 2])
+            for rows in attended.get(step + 2, []):
+                invert_sums(*rows)
+            if turn == 1 and head < last:
+                turn_q_and_k(head, 1)
+            for rows in attended.get(step, []):
+                attend(*rows)
+            if turn == 4 and head < last:
+                turn_q_and_k(head + 1, 0)
+            if turn == 6 and head == last - 1:
+                turn_q_and_k(last, 1)
+            if step in projected:
+                project_v(projected[step])
+            if step in turned_w:
+                turn_w(turned_w[step])

@@ -86,18 +86,16 @@ def tile_bloomattention_pa_kernel(tc, q, k, hidden_states, w_v, b_v, out):
         nc.sync.dma_start(out=hs_sb[:, 1:2], in_=hs_rows[:, 1:2])
         nc.sync.dma_start(out=w_sb[:, 0:4], in_=w_rows[:, 0:4])
         nc.sync.dma_start(out=w_sb[:, 4:8], in_=w_rows[:, 4:8])
+        bias_sb = inputs.tile([P, HIDDEN], BF16)
+        nc.sync.dma_start(out=bias_sb[:], in_=b_v.partition_broadcast(P))
         for heads in (middle, late):
             for c in range(2 * SPANS):
                 nc.sync.dma_start(out=k_sb[:, c, :, heads], in_=k_rows[:, c, :, heads])
             nc.sync.dma_start(out=q_sb[:, :, heads], in_=q_rows[:, :, heads])
-        bias_sb = inputs.tile([P, HIDDEN], BF16)
-        nc.scalar.dma_start(out=bias_sb[:], in_=b_v.partition_broadcast(P))
         out_rows = out.rearrange("b (a p) (h d) -> p (b a) h d", p=P, d=D)
 
-        ident_bf = consts.tile([P, P], BF16)
-        make_identity(nc, ident_bf[:])
-        ident_f32 = consts.tile([P, P], F32)
-        make_identity(nc, ident_f32[:])
+        earlier_i32 = consts.tile([P, 2, PLANE], I32)
+        nc.gpsimd.iota(earlier_i32[:], pattern=[[1, 2], [2, PLANE]], base=1 - 2 * SPAN, channel_multiplier=0)
         position_i32 = consts.tile([P, BLOCKS], I32)
         ahead_i32 = consts.tile([P, P], I32)
         for u in range(2):
@@ -106,8 +104,10 @@ def tile_bloomattention_pa_kernel(tc, q, k, hidden_states, w_v, b_v, out):
                 position_i32[plane, :], pattern=[[P, BLOCKS]], base=u - (SPAN - 1), channel_multiplier=2
             )
             nc.gpsimd.iota(ahead_i32[plane, :], pattern=[[1, P]], base=-u, channel_multiplier=-2)
-        earlier_i32 = consts.tile([P, 2, PLANE], I32)
-        nc.gpsimd.iota(earlier_i32[:], pattern=[[1, 2], [2, PLANE]], base=1 - 2 * SPAN, channel_multiplier=0)
+        ident_bf = consts.tile([P, P], BF16)
+        make_identity(nc, ident_bf[:])
+        ident_f32 = consts.tile([P, P], F32)
+        make_identity(nc, ident_f32[:])
         ones_bf = consts.tile([P, P], BF16)
         nc.gpsimd.memset(ones_bf[:], 1.0)
 
@@ -118,12 +118,35 @@ def tile_bloomattention_pa_kernel(tc, q, k, hidden_states, w_v, b_v, out):
                 e_tile = e_pool.tile([P, 2, PLANE * spans_seen(a)], BF16, name="e_%d_%d" % (parity, a))
                 e_tiles[parity].append(e_tile)
                 if columns_seen(a) < PLANE * spans_seen(a):
-                    nc.vector.memset(e_tile[:, :, columns_seen(a) :], 0.0)
+                    nc.gpsimd.memset(e_tile[:, :, columns_seen(a) :].bitcast(F32), 0.0)
+
+        earlier_rows = consts.tile([P, SPAN], BF16)
+        nc.vector.memset(earlier_rows[:], 0.0)
+        rests = [consts.tile([P, SPAN], F32, name="rest_%d" % part) for part in range(3)]
+        rounded = [consts.tile([P, SPAN], BF16, name="rounded_%d" % part) for part in range(2)]
+        nc.vector.tensor_scalar_mul(
+            out=rests[0][:], in0=earlier_i32[:].rearrange("p u z -> p (u z)"), scalar1=1.0 / SCALE
+        )
+
+        def split_off(part):
+            nc.vector.tensor_copy(out=rounded[part][:], in_=rests[part][:])
+            nc.vector.tensor_sub(out=rests[part + 1][:], in0=rests[part][:], in1=rounded[part][:])
+
+        def lay_out_earlier_rows():
+            for part in range(3):
+                row = slice(32 * part, 32 * part + 1)
+                nc.vector.tensor_copy(out=earlier_rows[row, :], in_=rests[part][row, :])
+
+        scaled_ident = consts.tile([P, HEADS, P], BF16)
+
+        def scale_identities(first, end):
+            for h in range(first, end):
+                nc.vector.tensor_scalar_mul(out=scaled_ident[:, h, :], in0=ident_bf[:], scalar1=2.0 ** (h + 1))
+
+        split_off(0)
 
         position = consts.tile([P, BLOCKS], F32)
         nc.vector.tensor_copy(out=position[:], in_=position_i32[:])
-        earlier = consts.tile([P, SPAN], F32)
-        nc.vector.tensor_copy(out=earlier[:], in_=earlier_i32[:].rearrange("p u z -> p (u z)"))
         mask = consts.tile([P, P], F32)
         nc.vector.tensor_scalar(
             out=mask[:], in0=ahead_i32[:], scalar1=0.0, scalar2=MASKED, op0=ALU.is_lt, op1=ALU.mult
@@ -138,23 +161,7 @@ def tile_bloomattention_pa_kernel(tc, q, k, hidden_states, w_v, b_v, out):
             in1=mask[:].unsqueeze(1).to_broadcast([P, BLOCKS, P]),
             op=ALU.add,
         )
-
-        def on_gpsimd(result, source, factor):
-            nc.gpsimd.tensor_scalar(out=result, in0=source, scalar1=factor, scalar2=0.0, op0=ALU.mult, op1=ALU.add)
-
-        earlier_rows = consts.tile([P, SPAN], BF16)
-        nc.gpsimd.memset(earlier_rows[:], 0.0)
-        rest = consts.tile([P, SPAN], F32, name="rest_0")
-        on_gpsimd(rest[:], earlier[:], 1.0 / SCALE)
-        for part in range(3):
-            row = slice(32 * part, 32 * part + 1)
-            exact = rest
-            if part < 2:
-                rounded = consts.tile([P, SPAN], BF16, name="rounded_%d" % part)
-                on_gpsimd(rounded[:], exact[:], 1.0)
-                rest = consts.tile([P, SPAN], F32, name="rest_%d" % (part + 1))
-                nc.gpsimd.tensor_tensor(out=rest[:], in0=exact[:], in1=rounded[:], op=ALU.subtract)
-            on_gpsimd(earlier_rows[row, :], exact[row, :], 1.0)
+        scale_identities(0, 1)
 
         hs_words = operands.tile([P, SPANS, PACK, SPANS, P], U32, align_bytes=64)
         hs_scales = operands.tile([P, SPANS, PACK, SPANS, P], U8, align_bytes=64)
@@ -210,7 +217,7 @@ def tile_bloomattention_pa_kernel(tc, q, k, hidden_states, w_v, b_v, out):
             for j in range(BLOCKS):
                 q_block = q_sb[:, BLOCKS * half + j, head]
                 if half == 1:
-                    nc.tensor.matmul(out=turned[:, 0, j, :], lhsT=q_block, rhs=ident_bf[:], start=True, stop=True)
+                    nc.tensor.matmul(out=turned[:, 0, j, :], lhsT=q_block, rhs=scaled_ident[:, h, :], start=True, stop=True)
                 else:
                     nc.tensor.transpose(turned[:, 0, j, :], q_block, ident_bf[:])
             q_turned = turned[:, 0]
@@ -220,9 +227,12 @@ def tile_bloomattention_pa_kernel(tc, q, k, hidden_states, w_v, b_v, out):
                 for f in range(2):
                     nc.tensor.transpose(turned[:, 1, 2 * u + f, :], k_sb[:, 2 * half + f, u, head], ident_bf[:])
             qk = turned_heads.tile([P, 2, BLOCKS, P], BF16, tag="qk")
-            nc.scalar.mul(out=qk[:, 0], in_=q_turned, mul=2.0 ** (h + 1))
-            copy_k = nc.vector.tensor_copy if (h, half) == (0, 0) else nc.scalar.copy
-            copy_k(out=qk[:, 1], in_=turned[:, 1])
+            if half == 1:
+                nc.scalar.copy(out=qk[:], in_=turned[:])
+            else:
+                nc.scalar.mul(out=qk[:, 0], in_=q_turned, mul=2.0 ** (h + 1))
+                copy_k = nc.vector.tensor_copy if h == 0 else nc.scalar.copy
+                copy_k(out=qk[:, 1], in_=turned[:, 1])
             qk_turned[(h, half)] = qk
 
         def project_v(h):
@@ -256,17 +266,17 @@ def tile_bloomattention_pa_kernel(tc, q, k, hidden_states, w_v, b_v, out):
         v_grouped = {}
         inverses = {}
         row_sums = {}
+        banks = {}
         scored = {}
         e_grouped = {}
         e_mx = {}
 
-        def scores(h, a):
-            minus_s = score_pool.tile([P, 2, PLANE * spans_seen(a)], F32, tag="minus_s")
-            lows = small.tile([P, SPANS], F32, tag="lows")
-            for g in range(spans_seen(a)):
+        def scores(h, a, g):
+            if g < spans_seen(a):
                 blocks = blocks_seen(a, g)
                 width = HALF * blocks
                 bank = psum_scores.tile([P, 2, PLANE], F32, tag="scores")
+                banks[(h, a, g)] = bank
                 if g < a // BLOCKS:
                     nc.tensor.matmul(
                         out=bank[:].rearrange("p u z -> p (u z)"),
@@ -293,22 +303,26 @@ def tile_bloomattention_pa_kernel(tc, q, k, hidden_states, w_v, b_v, out):
                     start=False,
                     stop=True,
                 )
+
+        def move_scores(h, a, g):
+            if g < spans_seen(a):
+                width = HALF * blocks_seen(a, g)
+                lowest = small.tile([P, 1], F32, tag="lowest")
+                if g == 0:
+                    minus_s = score_pool.tile([P, 2, PLANE * spans_seen(a)], F32, tag="minus_s")
+                    before = None
+                else:
+                    minus_s, earlier_lowest = scored[(h, a)]
+                    before = earlier_lowest[:, 0:1]
                 nc.vector.tensor_scalar(
                     out=minus_s[:, :, PLANE * g : PLANE * g + width],
-                    in0=bank[:, :, 0:width],
+                    in0=banks[(h, a, g)][:, :, 0:width],
                     scalar1=-SCALE * 0.5 ** (h + 1),
-                    scalar2=None,
+                    scalar2=before,
                     op0=ALU.mult,
                     op1=ALU.min,
-                    accum_out=lows[:, g : g + 1],
+                    accum_out=lowest[:],
                 )
-            scored[(h, a)] = (minus_s, lows)
-
-        def join_lows(h, a):
-            if spans_seen(a) == 2:
-                minus_s, lows = scored[(h, a)]
-                lowest = small.tile([P, 1], F32, tag="lowest")
-                nc.vector.tensor_tensor(out=lowest[:], in0=lows[:, 0:1], in1=lows[:, 1:2], op=ALU.min)
                 scored[(h, a)] = (minus_s, lowest)
 
         def exponentials(h, a):
@@ -379,7 +393,14 @@ def tile_bloomattention_pa_kernel(tc, q, k, hidden_states, w_v, b_v, out):
                 h, a = tiles[step]
                 if turn == 0:
                     row_sums[h] = small.tile([P, Q_TILES], F32, tag="sums", name="sums_%d" % h)
-                scores(h, a)
+                scores(h, a, 0)
+                scores(h, a, 1)
+                move_scores(h, a, 0)
+            if step == 1:
+                split_off(1)
+            if step == 2:
+                lay_out_earlier_rows()
+                scale_identities(1, HEADS)
             if step - 1 in projected:
                 quantise_v(projected[step - 1])
             if LAG_TURN <= step < len(tiles) + LAG_TURN:
@@ -392,13 +413,13 @@ def tile_bloomattention_pa_kernel(tc, q, k, hidden_states, w_v, b_v, out):
             if 0 <= piece - 1 < SPANS * PACK:
                 quantise_hidden_states(piece - 1)
             if step < len(tiles):
-                join_lows(h, a)
+                move_scores(h, a, 1)
                 exponentials(h, a)
             if step - 2 in turned_w:
                 quantise_w(turned_w[step - 2])
             for rows in attended.get(step + 2, []):
                 invert_sums(*rows)
-            if turn == 1 and head < last:
+            if turn == (1 if head > 0 else 0) and head < last:
                 turn_q_and_k(head, 1)
             for rows in attended.get(step, []):
                 attend(*rows)

@@ -170,14 +170,14 @@ def tile_bloomattention_pa_kernel(tc, q, k, hidden_states, w_v, b_v, out):
         v_words = operands.tile([P, HEADS, SPANS, D], U32, align_bytes=64)
         v_scales = operands.tile([P, HEADS, SPANS, D], U8, align_bytes=64)
 
-        def turn_rows(pairs, copy_out):
+        def turn_rows(pairs, banks_of, tag):
             count = pairs.shape[1]
-            turned = psum_turned.tile([P, count, 2, P], F32, tag="turned")
+            turned = banks_of.tile([P, count, 2, P], F32, tag=tag)
             for c in range(count):
                 for u in range(2):
                     nc.tensor.transpose(turned[:, c, u, :], pairs[:, c, u, :], ident_f32[:])
             grouped = stage.tile([P, count, P, PACK], BF16, tag="grouped", align_bytes=64)
-            copy_out(out=grouped[:].bitcast(F32), in_=turned[:].rearrange("p c u r -> p c r u"))
+            nc.scalar.copy(out=grouped[:].bitcast(F32), in_=turned[:].rearrange("p c u r -> p c r u"))
             return grouped
 
         def quantise(grouped, words, scales):
@@ -193,7 +193,7 @@ def tile_bloomattention_pa_kernel(tc, q, k, hidden_states, w_v, b_v, out):
         w_grouped = {}
 
         def turn_w(h):
-            w_grouped[h] = turn_rows(feature_pairs(w_sb[:, h, :]), nc.scalar.copy)
+            w_grouped[h] = turn_rows(feature_pairs(w_sb[:, h, :]), psum_turned, "turned")
 
         def quantise_w(h):
             quantise(w_grouped[h], w_words[:, h], w_scales[:, h])
@@ -202,8 +202,7 @@ def tile_bloomattention_pa_kernel(tc, q, k, hidden_states, w_v, b_v, out):
 
         def turn_hidden_states(piece):
             g, s = divmod(piece, PACK)
-            copy_out = nc.vector.tensor_copy if s % 2 == 0 else nc.scalar.copy
-            hs_grouped[piece] = turn_rows(feature_pairs(hs_sb[:, g, s, :]), copy_out)
+            hs_grouped[piece] = turn_rows(feature_pairs(hs_sb[:, g, s, :]), psum_products, "product")
 
         def quantise_hidden_states(piece):
             g, s = divmod(piece, PACK)
@@ -338,7 +337,7 @@ def tile_bloomattention_pa_kernel(tc, q, k, hidden_states, w_v, b_v, out):
 
         def turn_e(h, a):
             pairs = e_tiles[h % 2][a][:].bitcast(F32).rearrange("p u (g w) -> p g u w", w=P)
-            e_grouped[(h, a)] = turn_rows(pairs, nc.scalar.copy)
+            e_grouped[(h, a)] = turn_rows(pairs, psum_turned, "turned")
 
         def quantise_e(h, a):
             words = e_operands.tile([P, spans_seen(a), P], U32, tag="e_words", align_bytes=64)
@@ -381,7 +380,10 @@ def tile_bloomattention_pa_kernel(tc, q, k, hidden_states, w_v, b_v, out):
         turned_w = {max(Q_TILES * h - 1, HS_STEP + 6 + h): h for h in range(HEADS)}
         projected = {max(Q_TILES * h + 7, HS_STEP + 9): h for h in range(last)}
         projected[Q_TILES * last + 4] = last
-        attended = {Q_TILES * (h + 1) + 5: [(h, 0, BLOCKS), (h, BLOCKS, BLOCKS)] for h in range(last)}
+        attended = {Q_TILES * (h + 1) + 3: [(h, 0, BLOCKS)] for h in range(1, last)}
+        for h in range(last):
+            attended[Q_TILES * (h + 1) + 5] = [(h, BLOCKS, BLOCKS)]
+        attended[Q_TILES + 5] = [(0, 0, BLOCKS)] + attended[Q_TILES + 5]
         attended[Q_TILES * last + 7] = [(last, BLOCKS, BLOCKS)]
         attended[Q_TILES * last + 8] = [(last, 2, 2)]
         attended[Q_TILES * last + 10] = [(last, 0, 2)]

@@ -59,6 +59,7 @@ def tile_bloomattention_pa_kernel(tc, q, k, hidden_states, w_v, b_v, out):
         turned_heads = ctx.enter_context(tc.tile_pool(name="turned_heads", bufs=4))
         stage = ctx.enter_context(tc.tile_pool(name="stage", bufs=6))
         e_operands = ctx.enter_context(tc.tile_pool(name="e_operands", bufs=16))
+        v_stage = ctx.enter_context(tc.tile_pool(name="v_stage", bufs=2))
         small = ctx.enter_context(tc.tile_pool(name="small", bufs=6))
         score_pool = ctx.enter_context(tc.tile_pool(name="score_pool", bufs=4))
         results = ctx.enter_context(tc.tile_pool(name="results", bufs=4))
@@ -208,6 +209,7 @@ def tile_bloomattention_pa_kernel(tc, q, k, hidden_states, w_v, b_v, out):
             g, s = divmod(piece, PACK)
             quantise(hs_grouped[piece], hs_words[:, g, s], hs_scales[:, g, s])
 
+        k_by_matmul = [(0, 0), (0, 1), (1, 1)]
         qk_turned = {}
 
         def turn_q_and_k(h, half):
@@ -224,7 +226,11 @@ def tile_bloomattention_pa_kernel(tc, q, k, hidden_states, w_v, b_v, out):
                 turned = psum_turned.tile([P, 2, BLOCKS, P], BF16, tag="turned")
             for u in range(2):
                 for f in range(2):
-                    nc.tensor.transpose(turned[:, 1, 2 * u + f, :], k_sb[:, 2 * half + f, u, head], ident_bf[:])
+                    k_block = k_sb[:, 2 * half + f, u, head]
+                    if (h, half) in k_by_matmul:
+                        nc.tensor.matmul(out=turned[:, 1, 2 * u + f, :], lhsT=k_block, rhs=ident_bf[:], start=True, stop=True)
+                    else:
+                        nc.tensor.transpose(turned[:, 1, 2 * u + f, :], k_block, ident_bf[:])
             qk = turned_heads.tile([P, 2, BLOCKS, P], BF16, tag="qk")
             if half == 1:
                 nc.scalar.copy(out=qk[:], in_=turned[:])
@@ -234,30 +240,29 @@ def tile_bloomattention_pa_kernel(tc, q, k, hidden_states, w_v, b_v, out):
                 copy_k(out=qk[:, 1], in_=turned[:, 1])
             qk_turned[(h, half)] = qk
 
-        def project_v(h):
+        def project_v(h, g):
             head = slice(h * D, (h + 1) * D)
-            grouped = stage.tile([P, SPANS, D, PACK], BF16, tag="grouped", align_bytes=64)
-            for g in range(SPANS):
-                product = psum_products.tile([P, PACK, D], F32, tag="product")
-                for slot in range(PACK):
-                    s = 2 * (slot % 2) + slot // 2
-                    for c in range(SPANS):
-                        nc.tensor.matmul_mx(
-                            out=product[:, slot, :],
-                            lhsT=hs_words[:, g, s, c, :].bitcast(FP8X4),
-                            lhsT_scale=hs_scales[:, g, s, c, :],
-                            rhs=w_words[:, h, c, :].bitcast(FP8X4),
-                            rhs_scale=w_scales[:, h, c, :],
-                            start=(c == 0),
-                            stop=(c == SPANS - 1),
-                        )
-                nc.vector.tensor_tensor(
-                    out=grouped[:, g, :, :],
-                    in0=product[:].rearrange("p s d -> p d s"),
-                    in1=bias_sb[:, head].unsqueeze(2).to_broadcast([P, D, PACK]),
-                    op=ALU.add,
-                )
-            v_grouped[h] = grouped
+            if g == 0:
+                v_grouped[h] = v_stage.tile([P, SPANS, D, PACK], BF16, tag="v_grouped", align_bytes=64, name="v_%d" % h)
+            product = psum_products.tile([P, PACK, D], F32, tag="product")
+            for slot in range(PACK):
+                s = 2 * (slot % 2) + slot // 2
+                for c in range(SPANS):
+                    nc.tensor.matmul_mx(
+                        out=product[:, slot, :],
+                        lhsT=hs_words[:, g, s, c, :].bitcast(FP8X4),
+                        lhsT_scale=hs_scales[:, g, s, c, :],
+                        rhs=w_words[:, h, c, :].bitcast(FP8X4),
+                        rhs_scale=w_scales[:, h, c, :],
+                        start=(c == 0),
+                        stop=(c == SPANS - 1),
+                    )
+            nc.vector.tensor_tensor(
+                out=v_grouped[h][:, g, :, :],
+                in0=product[:].rearrange("p s d -> p d s"),
+                in1=bias_sb[:, head].unsqueeze(2).to_broadcast([P, D, PACK]),
+                op=ALU.add,
+            )
 
         def quantise_v(h):
             quantise(v_grouped[h], v_words[:, h], v_scales[:, h])
@@ -377,9 +382,13 @@ def tile_bloomattention_pa_kernel(tc, q, k, hidden_states, w_v, b_v, out):
         last = HEADS - 1
         tiles = [(h, a) for h in range(last) for a in range(Q_TILES)]
         tiles = tiles + [(last, a) for a in (4, 5, 6, 7, 3, 2, 1, 0)]
-        turned_w = {max(Q_TILES * h - 1, HS_STEP + 6 + h): h for h in range(HEADS)}
-        projected = {max(Q_TILES * h + 7, HS_STEP + 9): h for h in range(last)}
-        projected[Q_TILES * last + 4] = last
+        turned_w = {max(Q_TILES * h - 1, HS_STEP + 5 + h): h for h in range(HEADS)}
+        projected = {HS_STEP + 9: [(0, 0), (0, 1)], Q_TILES * last + 4: [(last, 0), (last, 1)]}
+        quantised_v = {HS_STEP + 10: 0, Q_TILES * last + 5: last}
+        for h in range(1, last):
+            projected[Q_TILES * h + 7] = [(h, 0)]
+            projected[Q_TILES * h + 8] = [(h, 1)]
+            quantised_v[Q_TILES * h + 9] = h
         attended = {Q_TILES * (h + 1) + 3: [(h, 0, BLOCKS)] for h in range(1, last)}
         for h in range(last):
             attended[Q_TILES * (h + 1) + 5] = [(h, BLOCKS, BLOCKS)]
@@ -403,8 +412,8 @@ def tile_bloomattention_pa_kernel(tc, q, k, hidden_states, w_v, b_v, out):
             if step == 2:
                 lay_out_earlier_rows()
                 scale_identities(1, HEADS)
-            if step - 1 in projected:
-                quantise_v(projected[step - 1])
+            if step in quantised_v:
+                quantise_v(quantised_v[step])
             if LAG_TURN <= step < len(tiles) + LAG_TURN:
                 turn_e(*tiles[step - LAG_TURN])
             piece = step - HS_STEP
@@ -429,7 +438,7 @@ def tile_bloomattention_pa_kernel(tc, q, k, hidden_states, w_v, b_v, out):
                 turn_q_and_k(head + 1, 0)
             if turn == 6 and head == last - 1:
                 turn_q_and_k(last, 1)
-            if step in projected:
-                project_v(projected[step])
+            for head_and_span in projected.get(step, []):
+                project_v(*head_and_span)
             if step in turned_w:
                 turn_w(turned_w[step])

@@ -63,9 +63,8 @@ def tile_bloomattention_pa_kernel(tc, q, k, hidden_states, w_v, b_v, out):
         small = ctx.enter_context(tc.tile_pool(name="small", bufs=6))
         score_pool = ctx.enter_context(tc.tile_pool(name="score_pool", bufs=4))
         results = ctx.enter_context(tc.tile_pool(name="results", bufs=4))
-        psum_scores = ctx.enter_context(tc.psum_pool(name="psum_scores", bufs=3))
-        psum_turned = ctx.enter_context(tc.psum_pool(name="psum_turned", bufs=3))
-        psum_products = ctx.enter_context(tc.psum_pool(name="psum_products", bufs=2))
+        psum_sums = ctx.enter_context(tc.psum_pool(name="psum_sums", bufs=4))
+        psum_turned = ctx.enter_context(tc.psum_pool(name="psum_turned", bufs=4))
 
         k_sb = inputs.tile([P, 2 * SPANS, 2, HIDDEN], BF16)
         k_rows = k.rearrange("b (c y u) h d -> y (b c) u (h d)", y=P, u=2)
@@ -203,7 +202,7 @@ def tile_bloomattention_pa_kernel(tc, q, k, hidden_states, w_v, b_v, out):
 
         def turn_hidden_states(piece):
             g, s = divmod(piece, PACK)
-            hs_grouped[piece] = turn_rows(feature_pairs(hs_sb[:, g, s, :]), psum_products, "product")
+            hs_grouped[piece] = turn_rows(feature_pairs(hs_sb[:, g, s, :]), psum_sums, "sums")
 
         def quantise_hidden_states(piece):
             g, s = divmod(piece, PACK)
@@ -244,7 +243,7 @@ def tile_bloomattention_pa_kernel(tc, q, k, hidden_states, w_v, b_v, out):
             head = slice(h * D, (h + 1) * D)
             if g == 0:
                 v_grouped[h] = v_stage.tile([P, SPANS, D, PACK], BF16, tag="v_grouped", align_bytes=64, name="v_%d" % h)
-            product = psum_products.tile([P, PACK, D], F32, tag="product")
+            product = psum_sums.tile([P, PACK, D], F32, tag="sums")
             for slot in range(PACK):
                 s = 2 * (slot % 2) + slot // 2
                 for c in range(SPANS):
@@ -279,7 +278,7 @@ def tile_bloomattention_pa_kernel(tc, q, k, hidden_states, w_v, b_v, out):
             if g < spans_seen(a):
                 blocks = blocks_seen(a, g)
                 width = HALF * blocks
-                bank = psum_scores.tile([P, 2, PLANE], F32, tag="scores")
+                bank = psum_sums.tile([P, 2, PLANE], F32, tag="sums")
                 banks[(h, a, g)] = bank
                 if g < a // BLOCKS:
                     nc.tensor.matmul(
@@ -357,7 +356,7 @@ def tile_bloomattention_pa_kernel(tc, q, k, hidden_states, w_v, b_v, out):
 
         def attend(h, first, count):
             upper = first // BLOCKS
-            product = psum_products.tile([P, BLOCKS, D], F32, tag="product")
+            product = psum_sums.tile([P, BLOCKS, D], F32, tag="sums")
             for j in range(count):
                 words, scales = e_mx[(h, first + j)]
                 for g in range(upper + 1):
@@ -383,16 +382,19 @@ def tile_bloomattention_pa_kernel(tc, q, k, hidden_states, w_v, b_v, out):
         tiles = [(h, a) for h in range(last) for a in range(Q_TILES)]
         tiles = tiles + [(last, a) for a in (4, 5, 6, 7, 3, 2, 1, 0)]
         turned_w = {max(Q_TILES * h - 1, HS_STEP + 5 + h): h for h in range(HEADS)}
-        projected = {HS_STEP + 9: [(0, 0), (0, 1)], Q_TILES * last + 4: [(last, 0), (last, 1)]}
+        projected = {HS_STEP + 8: [(0, 0)], HS_STEP + 9: [(0, 1)]}
+        projected[Q_TILES * last + 3] = [(last, 0)]
+        projected[Q_TILES * last + 4] = [(last, 1)]
         quantised_v = {HS_STEP + 10: 0, Q_TILES * last + 5: last}
         for h in range(1, last):
             projected[Q_TILES * h + 7] = [(h, 0)]
             projected[Q_TILES * h + 8] = [(h, 1)]
             quantised_v[Q_TILES * h + 9] = h
-        attended = {Q_TILES * (h + 1) + 3: [(h, 0, BLOCKS)] for h in range(1, last)}
+        attended = {}
         for h in range(last):
-            attended[Q_TILES * (h + 1) + 5] = [(h, BLOCKS, BLOCKS)]
-        attended[Q_TILES + 5] = [(0, 0, BLOCKS)] + attended[Q_TILES + 5]
+            attended[Q_TILES * (h + 1) + 5] = [(h, 0, BLOCKS)]
+            attended[Q_TILES * (h + 1) + 7] = [(h, BLOCKS, BLOCKS)]
+        attended[Q_TILES * last + 6] = attended[Q_TILES * last + 7]
         attended[Q_TILES * last + 7] = [(last, BLOCKS, BLOCKS)]
         attended[Q_TILES * last + 8] = [(last, 2, 2)]
         attended[Q_TILES * last + 10] = [(last, 0, 2)]
@@ -434,7 +436,7 @@ def tile_bloomattention_pa_kernel(tc, q, k, hidden_states, w_v, b_v, out):
                 turn_q_and_k(head, 1)
             for rows in attended.get(step, []):
                 attend(*rows)
-            if turn == 4 and head < last:
+            if turn == 3 and head < last:
                 turn_q_and_k(head + 1, 0)
             if turn == 6 and head == last - 1:
                 turn_q_and_k(last, 1)

@@ -111,6 +111,8 @@ def tile_bloomattention_pa_kernel(tc, q, k, hidden_states, w_v, b_v, out):
         ones_bf = consts.tile([P, P], BF16)
         nc.gpsimd.memset(ones_bf[:], 1.0)
 
+        zeros = consts.tile([P, 2, (PLANE - HALF) // 2], F32)
+        nc.vector.memset(zeros[:], 0.0)
         e_tiles = []
         for parity in range(2):
             e_tiles.append([])
@@ -118,7 +120,8 @@ def tile_bloomattention_pa_kernel(tc, q, k, hidden_states, w_v, b_v, out):
                 e_tile = e_pool.tile([P, 2, PLANE * spans_seen(a)], BF16, name="e_%d_%d" % (parity, a))
                 e_tiles[parity].append(e_tile)
                 if columns_seen(a) < PLANE * spans_seen(a):
-                    nc.gpsimd.memset(e_tile[:, :, columns_seen(a) :].bitcast(F32), 0.0)
+                    unseen = e_tile[:, :, columns_seen(a) :].bitcast(F32)
+                    nc.scalar.copy(out=unseen, in_=zeros[:, :, 0 : unseen.shape[2]])
 
         earlier_rows = consts.tile([P, SPAN], BF16)
         nc.vector.memset(earlier_rows[:], 0.0)

@@ -384,7 +384,7 @@ def tile_bloomattention_pa_kernel(tc, q, k, hidden_states, w_v, b_v, out):
         last = HEADS - 1
         tiles = [(h, a) for h in range(last) for a in range(Q_TILES)]
         tiles = tiles + [(last, a) for a in (4, 5, 6, 7, 3, 2, 1, 0)]
-        turned_w = {max(Q_TILES * h - 1, HS_STEP + 5 + h): h for h in range(HEADS)}
+        turned_w = {max(Q_TILES * h - 3, HS_STEP + 5 + h): h for h in range(HEADS)}
         projected = {HS_STEP + 8: [(0, 0)], HS_STEP + 9: [(0, 1)]}
         projected[Q_TILES * last + 3] = [(last, 0)]
         projected[Q_TILES * last + 4] = [(last, 1)]
@@ -412,10 +412,11 @@ def tile_bloomattention_pa_kernel(tc, q, k, hidden_states, w_v, b_v, out):
                 scores(h, a, 0)
                 scores(h, a, 1)
                 move_scores(h, a, 0)
-            if step == 1:
+            if step == 0:
                 split_off(1)
-            if step == 2:
+            if step == 1:
                 lay_out_earlier_rows()
+            if step == 2:
                 scale_identities(1, HEADS)
             if step in quantised_v:
                 quantise_v(quantised_v[step])
@@ -426,11 +427,11 @@ def tile_bloomattention_pa_kernel(tc, q, k, hidden_states, w_v, b_v, out):
                 turn_hidden_states(piece)
             if LAG_QUANTISE <= step < len(tiles) + LAG_QUANTISE:
                 quantise_e(*tiles[step - LAG_QUANTISE])
-            if 0 <= piece - 1 < SPANS * PACK:
-                quantise_hidden_states(piece - 1)
             if step < len(tiles):
                 move_scores(h, a, 1)
                 exponentials(h, a)
+            if 0 <= piece - 1 < SPANS * PACK:
+                quantise_hidden_states(piece - 1)
             if step - 2 in turned_w:
                 quantise_w(turned_w[step - 2])
             for rows in attended.get(step + 2, []):

import math
from contextlib import ExitStack

import concourse.mybir as mybir
from concourse.masks import make_identity

F32 = mybir.dt.float32
BF16 = mybir.dt.bfloat16
I32 = mybir.dt.int32
U32 = mybir.dt.uint32
U8 = mybir.dt.uint8
FP8X4 = mybir.dt.float8_e4m3fn_x4
ALU = mybir.AluOpType
ACT = mybir.ActivationFunctionType

P = 128
PACK = 4
SPAN = P * PACK
SEQ = 1024
HIDDEN = 1024
HEADS = 8
D = HIDDEN // HEADS
Q_TILES = SEQ // P
SPANS = SEQ // SPAN
BLOCKS = SPAN // P
HALF = P // 2
PLANE = SPAN // 2

SCALE = 1.0 / math.sqrt(D)
MASKED = -(2.0**25)

FLOPS = 2 * SEQ * HIDDEN * HIDDEN + 2 * (2 * HEADS * D * (SPAN * SPAN + SPAN * SEQ))

LAG_TURN = 2
HS_STEP = 2
LAG_QUANTISE = 3


def spans_seen(a):
    return a // BLOCKS + 1


def blocks_seen(a, g):
    return min(a + 1 - BLOCKS * g, BLOCKS)


def columns_seen(a):
    return HALF * (a + 1)


def tile_bloomattention_pa_kernel(tc, q, k, hidden_states, w_v, b_v, out):
    nc = tc.nc
    with ExitStack() as ctx:
        ctx.enter_context(tc.manual_schedule())
        inputs = ctx.enter_context(tc.tile_pool(name="inputs", bufs=1))
        consts = ctx.enter_context(tc.tile_pool(name="consts", bufs=1))
        operands = ctx.enter_context(tc.tile_pool(name="operands", bufs=1))
        e_pool = ctx.enter_context(tc.tile_pool(name="e_pool", bufs=1))
        turned_heads = ctx.enter_context(tc.tile_pool(name="turned_heads", bufs=4))
        stage = ctx.enter_context(tc.tile_pool(name="stage", bufs=6))
        e_operands = ctx.enter_context(tc.tile_pool(name="e_operands", bufs=16))
        v_stage = ctx.enter_context(tc.tile_pool(name="v_stage", bufs=2))
        small = ctx.enter_context(tc.tile_pool(name="small", bufs=6))
        score_pool = ctx.enter_context(tc.tile_pool(name="score_pool", bufs=4))
        results = ctx.enter_context(tc.tile_pool(name="results", bufs=4))
        psum_sums = ctx.enter_context(tc.psum_pool(name="psum_sums", bufs=4))
        psum_turned = ctx.enter_context(tc.psum_pool(name="psum_turned", bufs=4))

        k_sb = inputs.tile([P, 2 * SPANS, 2, HIDDEN], BF16)
        k_rows = k.rearrange("b (c y u) h d -> y (b c) u (h d)", y=P, u=2)
        q_sb = inputs.tile([P, Q_TILES, HIDDEN], BF16)
        q_rows = q.rearrange("b (a p) h d -> p (b a) (h d)", p=P)
        hs_sb = inputs.tile([P, SPANS, PACK, HIDDEN], BF16)
        hs_rows = hidden_states.rearrange("b (g p s) f -> p (b g) s f", p=P, s=PACK)
        w_sb = inputs.tile([P, HEADS, HIDDEN], BF16)
        w_rows = w_v.rearrange("(o p) f -> p o f", p=P)
        early = slice(0, 2 * D)
        middle = slice(2 * D, 4 * D)
        late = slice(4 * D, HIDDEN)
        for half in range(2):
            for c in range(2 * half, 2 * half + 2):
                nc.sync.dma_start(out=k_sb[:, c, :, early], in_=k_rows[:, c, :, early])
            tiles_of_half = slice(BLOCKS * half, BLOCKS * (half + 1))
            nc.sync.dma_start(out=q_sb[:, tiles_of_half, early], in_=q_rows[:, tiles_of_half, early])
        nc.sync.dma_start(out=hs_sb[:, 0:1], in_=hs_rows[:, 0:1])
        nc.sync.dma_start(out=hs_sb[:, 1:2], in_=hs_rows[:, 1:2])
        nc.sync.dma_start(out=w_sb[:, 0:4], in_=w_rows[:, 0:4])
        nc.sync.dma_start(out=w_sb[:, 4:8], in_=w_rows[:, 4:8])
        bias_sb = inputs.tile([P, HIDDEN], BF16)
        nc.sync.dma_start(out=bias_sb[:], in_=b_v.partition_broadcast(P))
        for heads in (middle, late):
            for c in range(2 * SPANS):
                nc.sync.dma_start(out=k_sb[:, c, :, heads], in_=k_rows[:, c, :, heads])
            nc.sync.dma_start(out=q_sb[:, :, heads], in_=q_rows[:, :, heads])
        out_rows = out.rearrange("b (a p) (h d) -> p (b a) h d", p=P, d=D)

        earlier_i32 = consts.tile([P, 2, PLANE], I32)
        nc.gpsimd.iota(earlier_i32[:], pattern=[[1, 2], [2, PLANE]], base=1 - 2 * SPAN, channel_multiplier=0)
        position_i32 = consts.tile([P, BLOCKS], I32)
        ahead_i32 = consts.tile([P, P], I32)
        for u in range(2):
            plane = slice(HALF * u, HALF * (u + 1))
            nc.gpsimd.iota(
                position_i32[plane, :], pattern=[[P, BLOCKS]], base=u - (SPAN - 1), channel_multiplier=2
            )
            nc.gpsimd.iota(ahead_i32[plane, :], pattern=[[1, P]], base=-u, channel_multiplier=-2)
        ident_bf = consts.tile([P, P], BF16)
        make_identity(nc, ident_bf[:])
        ident_f32 = consts.tile([P, P], F32)
        make_identity(nc, ident_f32[:])
        ones_bf = consts.tile([P, P], BF16)
        nc.gpsimd.memset(ones_bf[:], 1.0)

        zeros = consts.tile([P, 2, (PLANE - HALF) // 2], F32)
        nc.vector.memset(zeros[:], 0.0)
        e_tiles = []
        for parity in range(2):
            e_tiles.append([])
            for a in range(Q_TILES):
                e_tile = e_pool.tile([P, 2, PLANE * spans_seen(a)], BF16, name="e_%d_%d" % (parity, a))
                e_tiles[parity].append(e_tile)
                if columns_seen(a) < PLANE * spans_seen(a):
                    unseen = e_tile[:, :, columns_seen(a) :].bitcast(F32)
                    nc.scalar.copy(out=unseen, in_=zeros[:, :, 0 : unseen.shape[2]])

        earlier_rows = consts.tile([P, SPAN], BF16)
        nc.vector.memset(earlier_rows[:], 0.0)
        rests = [consts.tile([P, SPAN], F32, name="rest_%d" % part) for part in range(3)]
        rounded = [consts.tile([P, SPAN], BF16, name="rounded_%d" % part) for part in range(2)]
        nc.vector.tensor_scalar_mul(
            out=rests[0][:], in0=earlier_i32[:].rearrange("p u z -> p (u z)"), scalar1=1.0 / SCALE
        )

        def split_off(part):
            nc.vector.tensor_copy(out=rounded[part][:], in_=rests[part][:])
            nc.vector.tensor_sub(out=rests[part + 1][:], in0=rests[part][:], in1=rounded[part][:])

        def lay_out_earlier_rows():
            for part in range(3):
                row = slice(32 * part, 32 * part + 1)
                nc.vector.tensor_copy(out=earlier_rows[row, :], in_=rests[part][row, :])

        scaled_ident = consts.tile([P, HEADS, P], BF16)

        def scale_identities(first, end):
            for h in range(first, end):
                nc.vector.tensor_scalar_mul(out=scaled_ident[:, h, :], in0=ident_bf[:], scalar1=2.0 ** (h + 1))

        split_off(0)

        position = consts.tile([P, BLOCKS], F32)
        nc.vector.tensor_copy(out=position[:], in_=position_i32[:])
        mask = consts.tile([P, P], F32)
        nc.vector.tensor_scalar(
            out=mask[:], in0=ahead_i32[:], scalar1=0.0, scalar2=MASKED, op0=ALU.is_lt, op1=ALU.mult
        )
        added_terms = consts.tile([P, 2, BLOCKS, P], F32)
        nc.vector.tensor_scalar_mul(
            out=added_terms[:, 0], in0=position[:].unsqueeze(2).to_broadcast([P, BLOCKS, P]), scalar1=1.0 / SCALE
        )
        nc.vector.tensor_tensor(
            out=added_terms[:, 1],
            in0=added_terms[:, 0],
            in1=mask[:].unsqueeze(1).to_broadcast([P, BLOCKS, P]),
            op=ALU.add,
        )
        scale_identities(0, 1)

        hs_words = operands.tile([P, SPANS, PACK, SPANS, P], U32, align_bytes=64)
        hs_scales = operands.tile([P, SPANS, PACK, SPANS, P], U8, align_bytes=64)
        w_words = operands.tile([P, HEADS, SPANS, P], U32, align_bytes=64)
        w_scales = operands.tile([P, HEADS, SPANS, P], U8, align_bytes=64)
        v_words = operands.tile([P, HEADS, SPANS, D], U32, align_bytes=64)
        v_scales = operands.tile([P, HEADS, SPANS, D], U8, align_bytes=64)

        def turn_rows(pairs, banks_of, tag):
            count = pairs.shape[1]
            turned = banks_of.tile([P, count, 2, P], F32, tag=tag)
            for c in range(count):
                for u in range(2):
                    nc.tensor.transpose(turned[:, c, u, :], pairs[:, c, u, :], ident_f32[:])
            grouped = stage.tile([P, count, P, PACK], BF16, tag="grouped", align_bytes=64)
            nc.scalar.copy(out=grouped[:].bitcast(F32), in_=turned[:].rearrange("p c u r -> p c r u"))
            return grouped

        def quantise(grouped, words, scales):
            nc.vector.quantize_mx(
                out=words.rearrange("p c r -> p (c r)").bitcast(FP8X4),
                scales=scales.rearrange("p c r -> p (c r)"),
                in_=grouped[:].rearrange("p c r s -> p (c r s)"),
            )

        def feature_pairs(rows):
            return rows.bitcast(F32).rearrange("p (c u w) -> p c u w", c=SPANS, u=2)

        w_grouped = {}

        def turn_w(h):
            w_grouped[h] = turn_rows(feature_pairs(w_sb[:, h, :]), psum_turned, "turned")

        def quantise_w(h):
            quantise(w_grouped[h], w_words[:, h], w_scales[:, h])

        hs_grouped = {}

        def turn_hidden_states(piece):
            g, s = divmod(piece, PACK)
            hs_grouped[piece] = turn_rows(feature_pairs(hs_sb[:, g, s, :]), psum_sums, "sums")

        def quantise_hidden_states(piece):
            g, s = divmod(piece, PACK)
            quantise(hs_grouped[piece], hs_words[:, g, s], hs_scales[:, g, s])

        k_by_matmul = [(0, 0), (0, 1), (1, 1)]
        qk_turned = {}

        def turn_q_and_k(h, half):
            head = slice(h * D, (h + 1) * D)
            turned = psum_turned.tile([P, 2, BLOCKS, P], BF16, tag="turned")
            for j in range(BLOCKS):
                q_block = q_sb[:, BLOCKS * half + j, head]
                if half == 1:
                    nc.tensor.matmul(out=turned[:, 0, j, :], lhsT=q_block, rhs=scaled_ident[:, h, :], start=True, stop=True)
                else:
                    nc.tensor.transpose(turned[:, 0, j, :], q_block, ident_bf[:])
            q_turned = turned[:, 0]
            if (h, half) == (0, 0):
                turned = psum_turned.tile([P, 2, BLOCKS, P], BF16, tag="turned")
            for u in range(2):
                for f in range(2):
                    k_block = k_sb[:, 2 * half + f, u, head]
                    if (h, half) in k_by_matmul:
                        nc.tensor.matmul(out=turned[:, 1, 2 * u + f, :], lhsT=k_block, rhs=ident_bf[:], start=True, stop=True)
                    else:
                        nc.tensor.transpose(turned[:, 1, 2 * u + f, :], k_block, ident_bf[:])
            qk = turned_heads.tile([P, 2, BLOCKS, P], BF16, tag="qk")
            if half == 1:
                nc.scalar.copy(out=qk[:], in_=turned[:])
            else:
                nc.scalar.mul(out=qk[:, 0], in_=q_turned, mul=2.0 ** (h + 1))
                copy_k = nc.vector.tensor_copy if h == 0 else nc.scalar.copy
                copy_k(out=qk[:, 1], in_=turned[:, 1])
            qk_turned[(h, half)] = qk

        def project_v(h, g):
            head = slice(h * D, (h + 1) * D)
            if g == 0:
                v_grouped[h] = v_stage.tile([P, SPANS, D, PACK], BF16, tag="v_grouped", align_bytes=64, name="v_%d" % h)
            product = psum_sums.tile([P, PACK, D], F32, tag="sums")
            for slot in range(PACK):
                s = 2 * (slot % 2) + slot // 2
                for c in range(SPANS):
                    nc.tensor.matmul_mx(
                        out=product[:, slot, :],
                        lhsT=hs_words[:, g, s, c, :].bitcast(FP8X4),
                        lhsT_scale=hs_scales[:, g, s, c, :],
                        rhs=w_words[:, h, c, :].bitcast(FP8X4),
                        rhs_scale=w_scales[:, h, c, :],
                        start=(c == 0),
                        stop=(c == SPANS - 1),
                    )
            nc.vector.tensor_tensor(
                out=v_grouped[h][:, g, :, :],
                in0=product[:].rearrange("p s d -> p d s"),
                in1=bias_sb[:, head].unsqueeze(2).to_broadcast([P, D, PACK]),
                op=ALU.add,
            )

        def quantise_v(h):
            quantise(v_grouped[h], v_words[:, h], v_scales[:, h])

        v_grouped = {}
        inverses = {}
        row_sums = {}
        banks = {}
        scored = {}
        e_grouped = {}
        e_mx = {}

        def scores(h, a, g):
            if g < spans_seen(a):
                blocks = blocks_seen(a, g)
                width = HALF * blocks
                bank = psum_sums.tile([P, 2, PLANE], F32, tag="sums")
                banks[(h, a, g)] = bank
                if g < a // BLOCKS:
                    nc.tensor.matmul(
                        out=bank[:].rearrange("p u z -> p (u z)"),
                        lhsT=ones_bf[:],
                        rhs=earlier_rows[:],
                        start=True,
                        stop=False,
                    )
                else:
                    for block in range(blocks):
                        masked = 1 if block == a % BLOCKS else 0
                        nc.tensor.matmul(
                            out=bank[:, :, HALF * block : HALF * (block + 1)],
                            lhsT=added_terms[:, masked, block, :],
                            rhs=ident_f32[:].rearrange("p (u z) -> p u z", u=2),
                            is_transpose=True,
                            start=(block == 0),
                            stop=False,
                        )
                nc.tensor.matmul(
                    out=bank[:, :, 0:width],
                    lhsT=qk_turned[(h, a // BLOCKS)][:, 0, a % BLOCKS, :],
                    rhs=qk_turned[(h, g)][:, 1].rearrange("p (u f) y -> p u (f y)", u=2)[:, :, 0:width],
                    start=False,
                    stop=True,
                )

        def move_scores(h, a, g):
            if g < spans_seen(a):
                width = HALF * blocks_seen(a, g)
                lowest = small.tile([P, 1], F32, tag="lowest")
                if g == 0:
                    minus_s = score_pool.tile([P, 2, PLANE * spans_seen(a)], F32, tag="minus_s")
                    before = None
                else:
                    minus_s, earlier_lowest = scored[(h, a)]
                    before = earlier_lowest[:, 0:1]
                nc.vector.tensor_scalar(
                    out=minus_s[:, :, PLANE * g : PLANE * g + width],
                    in0=banks[(h, a, g)][:, :, 0:width],
                    scalar1=-SCALE * 0.5 ** (h + 1),
                    scalar2=before,
                    op0=ALU.mult,
                    op1=ALU.min,
                    accum_out=lowest[:],
                )
                scored[(h, a)] = (minus_s, lowest)

        def exponentials(h, a):
            minus_s, minus_top = scored[(h, a)]
            nc.scalar.activation(
                out=e_tiles[h % 2][a][:, :, 0 : columns_seen(a)],
                in_=minus_s[:, :, 0 : columns_seen(a)],
                func=ACT.Exp,
                bias=minus_top[:, 0:1],
                scale=-1.0,
                accum_out=row_sums[h][:, a : a + 1],
            )

        def turn_e(h, a):
            pairs = e_tiles[h % 2][a][:].bitcast(F32).rearrange("p u (g w) -> p g u w", w=P)
            e_grouped[(h, a)] = turn_rows(pairs, psum_turned, "turned")

        def quantise_e(h, a):
            words = e_operands.tile([P, spans_seen(a), P], U32, tag="e_words", align_bytes=64)
            scales = e_operands.tile([P, spans_seen(a), P], U8, tag="e_scales", align_bytes=64)
            quantise(e_grouped[(h, a)], words[:], scales[:])
            e_mx[(h, a)] = (words, scales)

        def invert_sums(h, first, count):
            inverse = small.tile([P, Q_TILES], F32, tag="inverse")
            nc.vector.reciprocal(out=inverse[:, 0:count], in_=row_sums[h][:, first : first + count])
            inverses[(h, first)] = inverse

        def attend(h, first, count):
            upper = first // BLOCKS
            product = psum_sums.tile([P, BLOCKS, D], F32, tag="sums")
            for j in range(count):
                words, scales = e_mx[(h, first + j)]
                for g in range(upper + 1):
                    nc.tensor.matmul_mx(
                        out=product[:, j, :],
                        lhsT=words[:, g, :].bitcast(FP8X4),
                        lhsT_scale=scales[:, g, :],
                        rhs=v_words[:, h, g, :].bitcast(FP8X4),
                        rhs_scale=v_scales[:, h, g, :],
                        start=(g == 0),
                        stop=(g == upper),
                    )
            result = results.tile([P, BLOCKS, D], F32, tag="result")
            nc.vector.tensor_tensor(
                out=result[:, 0:count],
                in0=product[:, 0:count],
                in1=inverses[(h, first)][:, 0:count].unsqueeze(2).to_broadcast([P, count, D]),
                op=ALU.mult,
            )
            nc.sync.dma_start(out=out_rows[:, first : first + count, h, :], in_=result[:, 0:count])

        last = HEADS - 1
        tiles = [(h, a) for h in range(last) for a in range(Q_TILES)]
        tiles = tiles + [(last, a) for a in (4, 5, 6, 7, 3, 2, 1, 0)]
        turned_w = {max(Q_TILES * h - 3, HS_STEP + 5 + h): h for h in range(HEADS)}
        projected = {HS_STEP + 8: [(0, 0)], HS_STEP + 9: [(0, 1)]}
        projected[Q_TILES * last + 3] = [(last, 0)]
        projected[Q_TILES * last + 4] = [(last, 1)]
        quantised_v = {HS_STEP + 10: 0, Q_TILES * last + 5: last}
        for h in range(1, last):
            projected[Q_TILES * h + 7] = [(h, 0)]
            projected[Q_TILES * h + 8] = [(h, 1)]
            quantised_v[Q_TILES * h + 9] = h
        attended = {}
        for h in range(last):
            attended[Q_TILES * (h + 1) + 5] = [(h, 0, BLOCKS)]
            attended[Q_TILES * (h + 1) + 7] = [(h, BLOCKS, BLOCKS)]
        attended[Q_TILES * last + 6] = attended[Q_TILES * last + 7]
        attended[Q_TILES * last + 7] = [(last, BLOCKS, BLOCKS)]
        attended[Q_TILES * last + 8] = [(last, 2, 2)]
        attended[Q_TILES * last + 10] = [(last, 0, 2)]

        turn_q_and_k(0, 0)
        for step in range(len(tiles) + Q_TILES):
            head, turn = divmod(step, Q_TILES)
            if step < len(tiles):
                h, a = tiles[step]
                if turn == 0:
                    row_sums[h] = small.tile([P, Q_TILES], F32, tag="sums", name="sums_%d" % h)
                scores(h, a, 0)
                scores(h, a, 1)
                move_scores(h, a, 0)
            if step == 0:
                split_off(1)
            if step == 1:
                lay_out_earlier_rows()
            if step == 2:
                scale_identities(1, HEADS)
            if step in quantised_v:
                quantise_v(quantised_v[step])
            if LAG_TURN <= step < len(tiles) + LAG_TURN:
                turn_e(*tiles[step - LAG_TURN])
            piece = step - HS_STEP
            if 0 <= piece < SPANS * PACK:
                turn_hidden_states(piece)
            if LAG_QUANTISE <= step < len(tiles) + LAG_QUANTISE:
                quantise_e(*tiles[step - LAG_QUANTISE])
            if step < len(tiles):
                move_scores(h, a, 1)
                exponentials(h, a)
            if 0 <= piece - 1 < SPANS * PACK:
                quantise_hidden_states(piece - 1)
            if step - 2 in turned_w:
                quantise_w(turned_w[step - 2])
            for rows in attended.get(step + 2, []):
                invert_sums(*rows)
            if turn == (1 if head > 0 else 0) and head < last:
                turn_q_and_k(head, 1)
            for rows in attended.get(step, []):
                attend(*rows)
            if turn == 3 and head < last:
                turn_q_and_k(head + 1, 0)
            if turn == 6 and head == last - 1:
                turn_q_and_k(last, 1)
            for head_and_span in projected.get(step, []):
                project_v(*head_and_span)
            if step in turned_w:
                turn_w(turned_w[step])
